import numpy as np
import ml_dtypes


def mxq(x, axis, fmt="e4m3"):
    dtype, down = {"e4m3": (ml_dtypes.float8_e4m3fn, 7), "e5m2": (ml_dtypes.float8_e5m2, 14)}[fmt]
    v = np.moveaxis(np.asarray(x, np.float32).astype(ml_dtypes.bfloat16).astype(np.float64), axis, -1)
    blocks = v.reshape(v.shape[:-1] + (-1, 32))
    amax = np.abs(blocks).max(-1, keepdims=True)
    byte = np.maximum(np.where(amax > 0, np.frexp(amax)[1] - 1 + 127, 0) - down, 1)
    scale = np.exp2(byte - 127.0)
    codes = (blocks / scale).astype(np.float32).astype(dtype).astype(np.float64)
    return np.moveaxis((codes * scale).reshape(v.shape), -1, axis)


BF16 = ml_dtypes.bfloat16


def bf(x):
    return np.asarray(x, np.float32).astype(BF16)


def f64(x):
    return np.asarray(x).astype(np.float64)


N, K, C, M, R, L = 4096, 512, 32, 16, 2, 8

LN_EPS = 1e-5


def layer_norm(x, w, b):
    mu = np.mean(x, axis=-1, keepdims=True)
    var = np.var(x, axis=-1, keepdims=True)
    return (x - mu) / np.sqrt(var + LN_EPS) * w + b


def l2_normalize(x, eps=1e-12):
    n = np.sqrt(np.sum(x * x, axis=-1, keepdims=True))
    return x / np.maximum(n, eps)


def clustered(rows, centres, a, b):
    return a * centres[np.random.randint(L, size=rows)] + b * np.random.standard_normal((rows, K))


def setup_inputs():
    cx = np.random.standard_normal((L, K))
    cv = np.random.standard_normal((L, K))
    x = clustered(N, cx, 0.7, 0.4) + 0.5 * np.random.standard_normal((N, 1))
    x_var = -1.0 + clustered(N, cv, 0.6, 0.5)
    prototypes = (clustered(C * M, cx, 0.7, 0.4) + 0.5 * np.random.standard_normal((C * M, 1))).reshape(C, M, K)
    proto_var = (-0.5 + clustered(C * M, cv, 0.6, 0.5)).reshape(C, M, K)
    return {"x": bf(x), "x_var": bf(x_var), "prototypes": bf(prototypes), "proto_var": bf(proto_var),
            "eps_x": bf(np.random.standard_normal((R, N, K))), "eps_p": bf(np.random.standard_normal((R, C, M, K))),
            "ln_w": bf(1.5 + 0.5 * np.random.standard_normal(K)), "ln_b": bf(0.5 * np.random.standard_normal(K))}


def reference(x, x_var, prototypes, proto_var, eps_x, eps_p, ln_w, ln_b):
    x, x_var, prototypes, proto_var = f64(x), f64(x_var), f64(prototypes), f64(proto_var)
    eps_x, eps_p, ln_w, ln_b = f64(eps_x), f64(eps_p), f64(ln_w), f64(ln_b)
    lamda = 1.0 / (K // 4)
    p_s = eps_p * np.exp(0.5 * proto_var) + prototypes
    p_s = l2_normalize(layer_norm(p_s, ln_w, ln_b))
    x_s = eps_x * np.exp(0.5 * x_var) + x
    x_s = l2_normalize(layer_norm(x_s, ln_w, ln_b))
    xv = np.exp(x_var)
    pv = np.exp(proto_var)
    xq = mxq(x_s, 2, "e4m3")
    pq = mxq(p_s, 3, "e4m3")
    sim = xq.reshape(R * N, K) @ pq.reshape(R * C * M, K).T
    sim = sim.reshape(R, N, R, C, M).transpose(0, 2, 1, 4, 3)
    sim = np.mean(sim.reshape((-1,) + sim.shape[2:]), axis=0)
    sim = np.transpose(sim, (2, 1, 0))
    cross = mxq(np.sqrt(xv), 1, "e4m3") @ mxq(np.sqrt(pv), 2, "e4m3").reshape(C * M, K).T
    cross = cross.T.reshape(C, M, N)
    w2 = (2.0 - 2.0 * sim
          + lamda * (np.sum(xv, axis=-1)
                     + np.sum(pv, axis=-1, keepdims=True)
                     - 2.0 * cross))
    return -np.transpose(w2, (2, 0, 1))

@@ -1,0 +1,335 @@
+from contextlib import ExitStack
+
+from concourse import mybir
+from concourse.masks import make_identity
+
+F32 = mybir.dt.float32
+BF16 = mybir.dt.bfloat16
+U32 = mybir.dt.uint32
+U8 = mybir.dt.uint8
+FP8X4 = mybir.dt.float8_e4m3fn_x4
+ALU = mybir.AluOpType
+ACT = mybir.ActivationFunctionType
+
+P = 128
+K = 512
+N_ROWS = 4096
+CM = 512
+R = 2
+GROUP = 4
+X_TILES = N_ROWS // P
+P_TILES = CM // P
+ITEMS = P_TILES + X_TILES
+LN_EPS = 1e-5
+LAMDA = 1.0 / 128.0
+
+FLOPS = 2 * (R * N_ROWS) * (R * CM) * K + 2 * N_ROWS * CM * K
+
+
+def tile_probprotoseghead_t_kernel(tc, x, x_var, prototypes, proto_var, eps_x, eps_p, ln_w, ln_b, out):
+    nc = tc.nc
+    with ExitStack() as ctx:
+        const = ctx.enter_context(tc.tile_pool(name="const", bufs=1))
+        io = ctx.enter_context(tc.tile_pool(name="io", bufs=3))
+        work = ctx.enter_context(tc.tile_pool(name="work", bufs=3))
+        small = ctx.enter_context(tc.tile_pool(name="small", bufs=4))
+        psc = ctx.enter_context(tc.psum_pool(name="psc", bufs=1))
+        psw = ctx.enter_context(tc.psum_pool(name="psw", bufs=2))
+        ctx.enter_context(tc.manual_schedule())
+
+        x_v = x.rearrange("(p t) k -> p t k", t=X_TILES)
+        xvar_v = x_var.rearrange("(p t) k -> p t k", t=X_TILES)
+        ex_v = [eps_x[r].rearrange("(p t) k -> p t k", t=X_TILES) for r in range(R)]
+        out_v = out.rearrange("(p t) c m -> p t (c m)", t=X_TILES)
+        p_v = prototypes.rearrange("(j c) m k -> (c m) j k", j=P_TILES)
+        pvar_v = proto_var.rearrange("(j c) m k -> (c m) j k", j=P_TILES)
+        ep_v = [eps_p[r].rearrange("(j c) m k -> (c m) j k", j=P_TILES) for r in range(R)]
+
+        wrow = const.tile([P, K], BF16, name="wrow")
+        brow = const.tile([P, K], BF16, name="brow")
+        nc.vector.memset(wrow[:], 0.0)
+        nc.vector.memset(brow[:], 0.0)
+        ones_bf = const.tile([P, P], BF16, name="ones_bf")
+        nc.vector.memset(ones_bf[:], 1.0)
+        ones_f = const.tile([P, P], F32, name="ones_f")
+        nc.vector.memset(ones_f[:], 1.0)
+        mhalf = const.tile([P, R], F32, name="mhalf")
+        nc.vector.memset(mhalf[:], -0.5)
+        ident_bf = const.tile([P, P], BF16, name="ident_bf")
+        make_identity(nc, ident_bf[:])
+        ident_f = const.tile([P, P], F32, name="ident_f")
+        make_identity(nc, ident_f[:])
+        w_ps = psc.tile([P, K], F32, name="w_ps")
+        b_ps = psc.tile([P, K], F32, name="b_ps")
+
+        col_term = const.tile([P, CM], F32, name="col_term")
+        p_codes = const.tile([P, R + 1, CM], U32, name="p_codes", align_bytes=64)
+        p_scales = const.tile([P, R + 1, CM], U8, name="p_scales", align_bytes=64)
+
+        groups = {}
+        st = {}
+
+        def load_group(g):
+            var_t = io.tile([P, GROUP, K], BF16, name="var_t", tag="var_t")
+            mean_t = io.tile([P, GROUP, K], BF16, name="mean_t", tag="mean_t")
+            eps_t = io.tile([P, R, GROUP, K], BF16, name="eps_t", tag="eps_t")
+            if g == 0:
+                srcs = (pvar_v, ep_v, p_v)
+                sl = slice(0, GROUP)
+            else:
+                srcs = (xvar_v, ex_v, x_v)
+                sl = slice((g - 1) * GROUP, g * GROUP)
+            nc.sync.dma_start(out=var_t[:], in_=srcs[0][:, sl, :])
+            for r in range(R):
+                nc.sync.dma_start(out=eps_t[:, r], in_=srcs[1][r][:, sl, :])
+            nc.sync.dma_start(out=mean_t[:], in_=srcs[2][:, sl, :])
+            groups[g] = (var_t, eps_t, mean_t)
+
+        def valid(i):
+            return 0 <= i < ITEMS
+
+        def is_x(i):
+            return P_TILES <= i < ITEMS
+
+        def pe_var_transposes(i):
+            var_t = groups[i // GROUP][0]
+            words = var_t[:, i % GROUP, :].bitcast(F32)
+            ts = psw.tile([P, K // 2], F32, name="ts", tag="ts")
+            for u in range(2):
+                nc.tensor.transpose(ts[:, u * P:(u + 1) * P], words[:, u * P:(u + 1) * P], ident_f[:])
+            st[i] = {"ts": ts}
+
+        def act_std(i):
+            d = st[i]
+            var_t = groups[i // GROUP][0]
+            s = work.tile([P, K], F32, name="s", tag="s")
+            nc.scalar.activation(out=s[:], in_=var_t[:, i % GROUP, :], func=ACT.Exp, scale=0.5)
+            junk = work.tile([P, K], BF16, name="junk", tag="junk", bufs=2)
+            svar = small.tile([P, 1], F32, name="svar", tag="svar", bufs=8)
+            nc.scalar.activation(out=junk[:], in_=var_t[:, i % GROUP, :], func=ACT.Exp, accum_out=svar[:])
+            gs = work.tile([P, K], BF16, name="gs", tag="gs", bufs=7, align_bytes=64)
+            nc.scalar.activation(
+                out=gs[:].rearrange("p (n u e) -> p n u e", u=2, e=2),
+                in_=d["ts"][:].bitcast(BF16).rearrange("p (u n e) -> p n u e", u=2, e=2),
+                func=ACT.Exp,
+                scale=0.5,
+            )
+            d["s"] = s
+            d["svar"] = svar
+            d["gs"] = gs
+
+        def pool_noise(i):
+            d = st[i]
+            eps_t = groups[i // GROUP][1]
+            v = work.tile([P, R, K], F32, name="v", tag="v", bufs=4)
+            nc.gpsimd.tensor_tensor(
+                out=v[:], in0=eps_t[:, :, i % GROUP, :], in1=d["s"][:].unsqueeze(1).to_broadcast([P, R, K]), op=ALU.mult
+            )
+            d["v"] = v
+            d["sv"] = small.tile([P, R], F32, name="sv", tag="sv")
+
+        def dve_mean(i, r):
+            d = st[i]
+            mean_t = groups[i // GROUP][2]
+            nc.vector.scalar_tensor_tensor(
+                out=d["v"][:, r, :], in0=d["v"][:, r, :], scalar=1.0, in1=mean_t[:, i % GROUP, :],
+                op0=ALU.mult, op1=ALU.add, accum_out=d["sv"][:, r:r + 1],
+            )
+
+        def dve_negmu(i):
+            d = st[i]
+            negmu = small.tile([P, R], F32, name="negmu", tag="negmu")
+            nc.vector.tensor_scalar(out=negmu[:], in0=d["sv"][:], scalar1=-1.0 / K, scalar2=None, op0=ALU.mult)
+            d["negmu"] = negmu
+
+        def act_var(i):
+            d = st[i]
+            ssq = small.tile([P, R], F32, name="ssq", tag="ssq")
+            for r in range(R):
+                junk = work.tile([P, K], BF16, name="junk", tag="junk", bufs=2)
+                nc.scalar.activation(
+                    out=junk[:], in_=d["v"][:, r, :], func=ACT.Square, bias=d["negmu"][:, r:r + 1], scale=1.0,
+                    accum_out=ssq[:, r:r + 1],
+                )
+            d["ssq"] = ssq
+
+        def pool_rstd(i):
+            d = st[i]
+            var = small.tile([P, R], F32, name="var", tag="var")
+            nc.gpsimd.tensor_scalar(out=var[:], in0=d["ssq"][:], scalar1=1.0 / K, scalar2=LN_EPS, op0=ALU.mult, op1=ALU.add)
+            rowc = small.tile([P, 1], F32, name="rowc", tag="rowc", bufs=8)
+            nc.gpsimd.tensor_scalar(
+                out=rowc[:], in0=d["svar"][:], scalar1=-LAMDA, scalar2=(-2.0 if i < P_TILES else 0.0),
+                op0=ALU.mult, op1=ALU.add,
+            )
+            d["rowc"] = rowc
+            rstd = small.tile([P, R], F32, name="rstd", tag="rstd")
+            nc.gpsimd.tensor_tensor(out=rstd[:], in0=var[:], in1=mhalf[:], op=ALU.pow)
+            d["rstd"] = rstd
+
+        def dve_gain(i, r):
+            d = st[i]
+            if r == 0:
+                d["u"] = work.tile([P, R, K], F32, name="u", tag="u")
+            nc.vector.scalar_tensor_tensor(
+                out=d["u"][:, r, :], in0=d["v"][:, r, :], scalar=d["negmu"][:, r:r + 1], in1=w_ps[:],
+                op0=ALU.add, op1=ALU.mult,
+            )
+
+        def dve_bias(i, r):
+            d = st[i]
+            nc.vector.scalar_tensor_tensor(
+                out=d["u"][:, r, :], in0=d["u"][:, r, :], scalar=d["rstd"][:, r:r + 1], in1=b_ps[:],
+                op0=ALU.mult, op1=ALU.add,
+            )
+
+        def act_norm(i):
+            d = st[i]
+            su2 = small.tile([P, R], F32, name="su2", tag="su2")
+            for r in range(R):
+                junk = work.tile([P, K], BF16, name="junk", tag="junk", bufs=2)
+                nc.scalar.activation(out=junk[:], in_=d["u"][:, r, :], func=ACT.Square, accum_out=su2[:, r:r + 1])
+            d["su2"] = su2
+
+        def pool_rnorm(i):
+            d = st[i]
+            cl = small.tile([P, R], F32, name="cl", tag="cl")
+            nc.gpsimd.tensor_scalar(
+                out=cl[:], in0=d["su2"][:], scalar1=1e-24, scalar2=(4.0 if i < P_TILES else 1.0), op0=ALU.max, op1=ALU.mult
+            )
+            dn = small.tile([P, R], F32, name="dn", tag="dn")
+            nc.gpsimd.tensor_tensor(out=dn[:], in0=cl[:], in1=mhalf[:], op=ALU.pow)
+            d["dn"] = dn
+
+        def dve_hat(i, r):
+            d = st[i]
+            if r == 0:
+                d["xh"] = work.tile([P, R, K], BF16, name="xh", tag="xh")
+            nc.vector.tensor_scalar(
+                out=d["xh"][:, r, :], in0=d["u"][:, r, :], scalar1=d["dn"][:, r:r + 1], scalar2=None, op0=ALU.mult
+            )
+
+        def pe_hat_transposes(i):
+            d = st[i]
+            tx = psw.tile([P, R, 4, P], BF16, name="tx", tag="tx")
+            for r in range(R):
+                for q in range(4):
+                    nc.tensor.transpose(tx[:, r, q, :], d["xh"][:, r, q * P:(q + 1) * P], ident_bf[:])
+            d["tx"] = tx
+
+        def column_term(i):
+            d = st[i]
+            crep = work.tile([P, P], F32, name="crep", tag="crep", bufs=2)
+            nc.vector.tensor_scalar(out=crep[:], in0=ones_f[:], scalar1=d["rowc"][:], scalar2=None, op0=ALU.mult)
+            tc_ps = psw.tile([P, K // 2], F32, name="tc_ps", tag="ts")
+            nc.tensor.transpose(tc_ps[:, 0:P], crep[:], ident_f[:])
+            nc.vector.tensor_copy(out=col_term[:, i * P:(i + 1) * P], in_=tc_ps[:, 0:P])
+
+        def act_regroup(i):
+            d = st[i]
+            gx = work.tile([P, R, P, 4], BF16, name="gx", tag="gx", align_bytes=64)
+            nc.scalar.copy(out=gx[:], in_=d["tx"][:].rearrange("p r q n -> p r n q"))
+            d["gx"] = gx
+
+        def dve_quantise(i):
+            d = st[i]
+            if i < P_TILES:
+                cols = slice(i * P, (i + 1) * P)
+                nc.vector.tensor_scalar(out=d["gs"][:], in0=d["gs"][:], scalar1=2.0 ** -6, scalar2=None, op0=ALU.mult)
+                for r in range(R):
+                    nc.vector.quantize_mx(
+                        out=p_codes[:, r, cols].bitcast(FP8X4), scales=p_scales[:, r, cols],
+                        in_=d["gx"][:, r].rearrange("p n q -> p (n q)"),
+                    )
+                nc.vector.quantize_mx(out=p_codes[:, R, cols].bitcast(FP8X4), scales=p_scales[:, R, cols], in_=d["gs"][:])
+            else:
+                codes = work.tile([P, (R + 1) * P], U32, name="codes", tag="codes", align_bytes=64)
+                scales = work.tile([P, (R + 1) * P], U8, name="scales", tag="scales", align_bytes=64)
+                nc.vector.quantize_mx(
+                    out=codes[:, 0:R * P].bitcast(FP8X4), scales=scales[:, 0:R * P],
+                    in_=d["gx"][:].rearrange("p r n q -> p (r n q)"),
+                )
+                nc.vector.quantize_mx(
+                    out=codes[:, R * P:(R + 1) * P].bitcast(FP8X4), scales=scales[:, R * P:(R + 1) * P], in_=d["gs"][:]
+                )
+                d["codes"] = codes
+                d["scales"] = scales
+
+        def pe_products(i):
+            d = st[i]
+            acc = psw.tile([P, CM], F32, name="acc", tag="acc")
+            passes = [(r, b) for r in range(R) for b in range(R)] + [(R, R)]
+            for n, (a, b) in enumerate(passes):
+                nc.tensor.matmul_mx(
+                    out=acc[:],
+                    lhsT=d["codes"][:, a * P:(a + 1) * P].bitcast(FP8X4),
+                    lhsT_scale=d["scales"][:, a * P:(a + 1) * P],
+                    rhs=p_codes[:, b, :].bitcast(FP8X4),
+                    rhs_scale=p_scales[:, b, :],
+                    start=(n == 0),
+                    stop=(n == len(passes) - 1),
+                )
+            d["acc"] = acc
+
+        def dve_output(i):
+            d = st[i]
+            t = i - P_TILES
+            if t % 2 == 0:
+                st["o"] = work.tile([P, 2, CM], F32, name="o", tag="o")
+            o = st["o"]
+            nc.vector.scalar_tensor_tensor(
+                out=o[:, t % 2, :], in0=d["acc"][:], scalar=d["rowc"][:], in1=col_term[:], op0=ALU.add, op1=ALU.add
+            )
+            if t % 2 == 1:
+                nc.sync.dma_start(out=out_v[:, t - 1:t + 1, :], in_=o[:])
+
+        n_groups = ITEMS // GROUP
+        load_group(0)
+        nc.sync.dma_start(out=wrow[0:1, :], in_=ln_w.unsqueeze(0))
+        nc.sync.dma_start(out=brow[0:1, :], in_=ln_b.unsqueeze(0))
+        load_group(1)
+        for j in range(-2, ITEMS + 4):
+            if valid(j + 2) and (j + 2) % GROUP == 0 and (j + 2) // GROUP + 2 < n_groups:
+                load_group((j + 2) // GROUP + 2)
+            if valid(j + 2):
+                pe_var_transposes(j + 2)
+            if j == -1:
+                nc.tensor.matmul(w_ps[:], lhsT=ones_bf[:], rhs=wrow[:], start=True, stop=True)
+                nc.tensor.matmul(b_ps[:], lhsT=ones_bf[:], rhs=brow[:], start=True, stop=True)
+            if is_x(j - 4):
+                pe_products(j - 4)
+            if valid(j - 1):
+                pool_rstd(j - 1)
+            if valid(j - 2):
+                act_norm(j - 2)
+                pool_rnorm(j - 2)
+            if valid(j + 1):
+                pool_noise(j + 1)
+            if valid(j - 3):
+                act_regroup(j - 3)
+            if valid(j + 2):
+                act_std(j + 2)
+            for r in range(R):
+                if valid(j):
+                    dve_mean(j, r)
+                if valid(j - 1):
+                    dve_gain(j - 1, r)
+            if valid(j):
+                dve_negmu(j)
+            if valid(j - 1):
+                dve_bias(j - 1, 0)
+            if is_x(j - 4):
+                dve_output(j - 4)
+            if valid(j - 1):
+                dve_bias(j - 1, 1)
+            if valid(j):
+                act_var(j)
+            if valid(j - 2):
+                dve_hat(j - 2, 0)
+            if valid(j - 3):
+                dve_quantise(j - 3)
+            if valid(j - 2):
+                dve_hat(j - 2, 1)
+                pe_hat_transposes(j - 2)
+                if j - 2 < P_TILES:
+                    column_term(j - 2)

@@ -94,7 +94,7 @@ def tile_probprotoseghead_t_kernel(tc, x, x_var, prototypes, proto_var, eps_x, e
         def pe_var_transposes(i):
             var_t = groups[i // GROUP][0]
             words = var_t[:, i % GROUP, :].bitcast(F32)
-            ts = psw.tile([P, K // 2], F32, name="ts", tag="ts")
+            ts = psc.tile([P, K // 2], F32, name="ts", tag="ts")
             for u in range(2):
                 nc.tensor.transpose(ts[:, u * P:(u + 1) * P], words[:, u * P:(u + 1) * P], ident_f[:])
             st[i] = {"ts": ts}
@@ -118,11 +118,17 @@ def tile_probprotoseghead_t_kernel(tc, x, x_var, prototypes, proto_var, eps_x, e
             d["svar"] = svar
             d["gs"] = gs
 
-        def pool_noise(i):
+        def pe_mean_copy(i):
+            mean_t = groups[i // GROUP][2]
+            xps = psw.tile([P, K], F32, name="xps", tag="xps")
+            nc.tensor.matmul(xps[:], lhsT=ident_bf[:], rhs=mean_t[:, i % GROUP, :], start=True, stop=True)
+            st[i]["xps"] = xps
+
+        def dve_noise(i):
             d = st[i]
             eps_t = groups[i // GROUP][1]
-            v = work.tile([P, R, K], F32, name="v", tag="v", bufs=4)
-            nc.gpsimd.tensor_tensor(
+            v = work.tile([P, R, K], F32, name="v", tag="v", bufs=3)
+            nc.vector.tensor_tensor(
                 out=v[:], in0=eps_t[:, :, i % GROUP, :], in1=d["s"][:].unsqueeze(1).to_broadcast([P, R, K]), op=ALU.mult
             )
             d["v"] = v
@@ -130,16 +136,15 @@ def tile_probprotoseghead_t_kernel(tc, x, x_var, prototypes, proto_var, eps_x, e
 
         def dve_mean(i, r):
             d = st[i]
-            mean_t = groups[i // GROUP][2]
             nc.vector.scalar_tensor_tensor(
-                out=d["v"][:, r, :], in0=d["v"][:, r, :], scalar=1.0, in1=mean_t[:, i % GROUP, :],
+                out=d["v"][:, r, :], in0=d["v"][:, r, :], scalar=1.0, in1=d["xps"][:],
                 op0=ALU.mult, op1=ALU.add, accum_out=d["sv"][:, r:r + 1],
             )
 
-        def dve_negmu(i):
+        def pool_negmu(i):
             d = st[i]
             negmu = small.tile([P, R], F32, name="negmu", tag="negmu")
-            nc.vector.tensor_scalar(out=negmu[:], in0=d["sv"][:], scalar1=-1.0 / K, scalar2=None, op0=ALU.mult)
+            nc.gpsimd.tensor_scalar(out=negmu[:], in0=d["sv"][:], scalar1=-1.0 / K, scalar2=0.0, op0=ALU.mult, op1=ALU.add)
             d["negmu"] = negmu
 
         def act_var(i):
@@ -170,7 +175,7 @@ def tile_probprotoseghead_t_kernel(tc, x, x_var, prototypes, proto_var, eps_x, e
         def dve_gain(i, r):
             d = st[i]
             if r == 0:
-                d["u"] = work.tile([P, R, K], F32, name="u", tag="u")
+                d["u"] = work.tile([P, R, K], F32, name="u", tag="u", bufs=4)
             nc.vector.scalar_tensor_tensor(
                 out=d["u"][:, r, :], in0=d["v"][:, r, :], scalar=d["negmu"][:, r:r + 1], in1=w_ps[:],
                 op0=ALU.add, op1=ALU.mult,
@@ -201,12 +206,12 @@ def tile_probprotoseghead_t_kernel(tc, x, x_var, prototypes, proto_var, eps_x, e
             nc.gpsimd.tensor_tensor(out=dn[:], in0=cl[:], in1=mhalf[:], op=ALU.pow)
             d["dn"] = dn
 
-        def dve_hat(i, r):
+        def pool_hat(i, r):
             d = st[i]
             if r == 0:
                 d["xh"] = work.tile([P, R, K], BF16, name="xh", tag="xh")
-            nc.vector.tensor_scalar(
-                out=d["xh"][:, r, :], in0=d["u"][:, r, :], scalar1=d["dn"][:, r:r + 1], scalar2=None, op0=ALU.mult
+            nc.gpsimd.tensor_scalar(
+                out=d["xh"][:, r, :], in0=d["u"][:, r, :], scalar1=d["dn"][:, r:r + 1], scalar2=0.0, op0=ALU.mult, op1=ALU.add
             )
 
         def pe_hat_transposes(i):
@@ -217,13 +222,16 @@ def tile_probprotoseghead_t_kernel(tc, x, x_var, prototypes, proto_var, eps_x, e
                     nc.tensor.transpose(tx[:, r, q, :], d["xh"][:, r, q * P:(q + 1) * P], ident_bf[:])
             d["tx"] = tx
 
-        def column_term(i):
+        def column_rep(i):
             d = st[i]
             crep = work.tile([P, P], F32, name="crep", tag="crep", bufs=2)
             nc.vector.tensor_scalar(out=crep[:], in0=ones_f[:], scalar1=d["rowc"][:], scalar2=None, op0=ALU.mult)
-            tc_ps = psw.tile([P, K // 2], F32, name="tc_ps", tag="ts")
+            tc_ps = psc.tile([P, K // 2], F32, name="tc_ps", tag="ts")
             nc.tensor.transpose(tc_ps[:, 0:P], crep[:], ident_f[:])
-            nc.vector.tensor_copy(out=col_term[:, i * P:(i + 1) * P], in_=tc_ps[:, 0:P])
+            d["tc_ps"] = tc_ps
+
+        def column_copy(i):
+            nc.vector.tensor_copy(out=col_term[:, i * P:(i + 1) * P], in_=st[i]["tc_ps"][:, 0:P])
 
         def act_regroup(i):
             d = st[i]
@@ -257,7 +265,7 @@ def tile_probprotoseghead_t_kernel(tc, x, x_var, prototypes, proto_var, eps_x, e
 
         def pe_products(i):
             d = st[i]
-            acc = psw.tile([P, CM], F32, name="acc", tag="acc")
+            acc = psc.tile([P, CM], F32, name="acc", tag="acc")
             passes = [(r, b) for r in range(R) for b in range(R)] + [(R, R)]
             for n, (a, b) in enumerate(passes):
                 nc.tensor.matmul_mx(
@@ -288,14 +296,19 @@ def tile_probprotoseghead_t_kernel(tc, x, x_var, prototypes, proto_var, eps_x, e
         nc.sync.dma_start(out=wrow[0:1, :], in_=ln_w.unsqueeze(0))
         nc.sync.dma_start(out=brow[0:1, :], in_=ln_b.unsqueeze(0))
         load_group(1)
-        for j in range(-2, ITEMS + 4):
-            if valid(j + 2) and (j + 2) % GROUP == 0 and (j + 2) // GROUP + 2 < n_groups:
-                load_group((j + 2) // GROUP + 2)
-            if valid(j + 2):
-                pe_var_transposes(j + 2)
+        for j in range(-1, ITEMS + 4):
+            if valid(j + 1) and (j + 1) % GROUP == 0 and (j + 1) // GROUP + 2 < n_groups:
+                load_group((j + 1) // GROUP + 2)
+            if valid(j + 1):
+                pe_var_transposes(j + 1)
+                pe_mean_copy(j + 1)
             if j == -1:
                 nc.tensor.matmul(w_ps[:], lhsT=ones_bf[:], rhs=wrow[:], start=True, stop=True)
                 nc.tensor.matmul(b_ps[:], lhsT=ones_bf[:], rhs=brow[:], start=True, stop=True)
+            if valid(j):
+                dve_noise(j)
+            if valid(j - 4):
+                dve_quantise(j - 4)
             if is_x(j - 4):
                 pe_products(j - 4)
             if valid(j - 1):
@@ -304,32 +317,27 @@ def tile_probprotoseghead_t_kernel(tc, x, x_var, prototypes, proto_var, eps_x, e
                 act_norm(j - 2)
                 pool_rnorm(j - 2)
             if valid(j + 1):
-                pool_noise(j + 1)
+                act_std(j + 1)
             if valid(j - 3):
                 act_regroup(j - 3)
-            if valid(j + 2):
-                act_std(j + 2)
-            for r in range(R):
-                if valid(j):
-                    dve_mean(j, r)
-                if valid(j - 1):
-                    dve_gain(j - 1, r)
             if valid(j):
-                dve_negmu(j)
+                dve_mean(j, 0)
+                dve_mean(j, 1)
+                pool_negmu(j)
+            if 0 <= j - 2 < P_TILES:
+                column_rep(j - 2)
+            if valid(j - 2):
+                pool_hat(j - 2, 0)
+                pool_hat(j - 2, 1)
+                pe_hat_transposes(j - 2)
             if valid(j - 1):
+                dve_gain(j - 1, 0)
+                dve_gain(j - 1, 1)
                 dve_bias(j - 1, 0)
+                dve_bias(j - 1, 1)
             if is_x(j - 4):
                 dve_output(j - 4)
-            if valid(j - 1):
-                dve_bias(j - 1, 1)
+            if 0 <= j - 2 < P_TILES:
+                column_copy(j - 2)
             if valid(j):
                 act_var(j)
-            if valid(j - 2):
-                dve_hat(j - 2, 0)
-            if valid(j - 3):
-                dve_quantise(j - 3)
-            if valid(j - 2):
-                dve_hat(j - 2, 1)
-                pe_hat_transposes(j - 2)
-                if j - 2 < P_TILES:
-                    column_term(j - 2)

@@ -53,7 +53,7 @@ def tile_probprotoseghead_t_kernel(tc, x, x_var, prototypes, proto_var, eps_x, e
         nc.vector.memset(ones_bf[:], 1.0)
         ones_f = const.tile([P, P], F32, name="ones_f")
         nc.vector.memset(ones_f[:], 1.0)
-        mhalf = const.tile([P, R], F32, name="mhalf")
+        mhalf = const.tile([P, 2 * R], F32, name="mhalf")
         nc.vector.memset(mhalf[:], -0.5)
         ident_bf = const.tile([P, P], BF16, name="ident_bf")
         make_identity(nc, ident_bf[:])
@@ -124,11 +124,11 @@ def tile_probprotoseghead_t_kernel(tc, x, x_var, prototypes, proto_var, eps_x, e
             nc.tensor.matmul(xps[:], lhsT=ident_bf[:], rhs=mean_t[:, i % GROUP, :], start=True, stop=True)
             st[i]["xps"] = xps
 
-        def dve_noise(i):
+        def pool_noise(i):
             d = st[i]
             eps_t = groups[i // GROUP][1]
-            v = work.tile([P, R, K], F32, name="v", tag="v", bufs=3)
-            nc.vector.tensor_tensor(
+            v = work.tile([P, R, K], F32, name="v", tag="v", bufs=4)
+            nc.gpsimd.tensor_tensor(
                 out=v[:], in0=eps_t[:, :, i % GROUP, :], in1=d["s"][:].unsqueeze(1).to_broadcast([P, R, K]), op=ALU.mult
             )
             d["v"] = v
@@ -141,10 +141,10 @@ def tile_probprotoseghead_t_kernel(tc, x, x_var, prototypes, proto_var, eps_x, e
                 op0=ALU.mult, op1=ALU.add, accum_out=d["sv"][:, r:r + 1],
             )
 
-        def pool_negmu(i):
+        def act_negmu(i):
             d = st[i]
             negmu = small.tile([P, R], F32, name="negmu", tag="negmu")
-            nc.gpsimd.tensor_scalar(out=negmu[:], in0=d["sv"][:], scalar1=-1.0 / K, scalar2=0.0, op0=ALU.mult, op1=ALU.add)
+            nc.scalar.mul(out=negmu[:], in_=d["sv"][:], mul=-1.0 / K)
             d["negmu"] = negmu
 
         def act_var(i):
@@ -158,19 +158,34 @@ def tile_probprotoseghead_t_kernel(tc, x, x_var, prototypes, proto_var, eps_x, e
                 )
             d["ssq"] = ssq
 
-        def pool_rstd(i):
-            d = st[i]
-            var = small.tile([P, R], F32, name="var", tag="var")
-            nc.gpsimd.tensor_scalar(out=var[:], in0=d["ssq"][:], scalar1=1.0 / K, scalar2=LN_EPS, op0=ALU.mult, op1=ALU.add)
-            rowc = small.tile([P, 1], F32, name="rowc", tag="rowc", bufs=8)
-            nc.gpsimd.tensor_scalar(
-                out=rowc[:], in0=d["svar"][:], scalar1=-LAMDA, scalar2=(-2.0 if i < P_TILES else 0.0),
-                op0=ALU.mult, op1=ALU.add,
-            )
-            d["rowc"] = rowc
-            rstd = small.tile([P, R], F32, name="rstd", tag="rstd")
-            nc.gpsimd.tensor_tensor(out=rstd[:], in0=var[:], in1=mhalf[:], op=ALU.pow)
-            d["rstd"] = rstd
+        def roots(i_var, i_norm):
+            pin = small.tile([P, 2 * R], F32, name="pin", tag="pin")
+            if valid(i_var):
+                d = st[i_var]
+                rowc = small.tile([P, 1], F32, name="rowc", tag="rowc", bufs=8)
+                nc.vector.tensor_scalar(
+                    out=rowc[:], in0=d["svar"][:], scalar1=-LAMDA, scalar2=(-2.0 if i_var < P_TILES else 0.0),
+                    op0=ALU.mult, op1=ALU.add,
+                )
+                d["rowc"] = rowc
+                nc.vector.tensor_scalar(
+                    out=pin[:, 0:R], in0=d["ssq"][:], scalar1=1.0 / K, scalar2=LN_EPS, op0=ALU.mult, op1=ALU.add
+                )
+            else:
+                nc.vector.memset(pin[:, 0:R], 1.0)
+            if valid(i_norm):
+                nc.vector.tensor_scalar(
+                    out=pin[:, R:2 * R], in0=st[i_norm]["su2"][:], scalar1=1e-24,
+                    scalar2=(4.0 if i_norm < P_TILES else 1.0), op0=ALU.max, op1=ALU.mult,
+                )
+            else:
+                nc.vector.memset(pin[:, R:2 * R], 1.0)
+            pout = small.tile([P, 2 * R], F32, name="pout", tag="pout", bufs=6)
+            nc.gpsimd.tensor_tensor(out=pout[:], in0=pin[:], in1=mhalf[:], op=ALU.pow)
+            if valid(i_var):
+                st[i_var]["rstd"] = pout[:, 0:R]
+            if valid(i_norm):
+                st[i_norm]["dn"] = pout[:, R:2 * R]
 
         def dve_gain(i, r):
             d = st[i]
@@ -196,22 +211,12 @@ def tile_probprotoseghead_t_kernel(tc, x, x_var, prototypes, proto_var, eps_x, e
                 nc.scalar.activation(out=junk[:], in_=d["u"][:, r, :], func=ACT.Square, accum_out=su2[:, r:r + 1])
             d["su2"] = su2
 
-        def pool_rnorm(i):
-            d = st[i]
-            cl = small.tile([P, R], F32, name="cl", tag="cl")
-            nc.gpsimd.tensor_scalar(
-                out=cl[:], in0=d["su2"][:], scalar1=1e-24, scalar2=(4.0 if i < P_TILES else 1.0), op0=ALU.max, op1=ALU.mult
-            )
-            dn = small.tile([P, R], F32, name="dn", tag="dn")
-            nc.gpsimd.tensor_tensor(out=dn[:], in0=cl[:], in1=mhalf[:], op=ALU.pow)
-            d["dn"] = dn
-
-        def pool_hat(i, r):
+        def dve_hat(i, r):
             d = st[i]
             if r == 0:
                 d["xh"] = work.tile([P, R, K], BF16, name="xh", tag="xh")
-            nc.gpsimd.tensor_scalar(
-                out=d["xh"][:, r, :], in0=d["u"][:, r, :], scalar1=d["dn"][:, r:r + 1], scalar2=0.0, op0=ALU.mult, op1=ALU.add
+            nc.vector.tensor_scalar(
+                out=d["xh"][:, r, :], in0=d["u"][:, r, :], scalar1=d["dn"][:, r:r + 1], scalar2=None, op0=ALU.mult
             )
 
         def pe_hat_transposes(i):
@@ -299,37 +304,34 @@ def tile_probprotoseghead_t_kernel(tc, x, x_var, prototypes, proto_var, eps_x, e
         for j in range(-1, ITEMS + 4):
             if valid(j + 1) and (j + 1) % GROUP == 0 and (j + 1) // GROUP + 2 < n_groups:
                 load_group((j + 1) // GROUP + 2)
+            if valid(j - 2):
+                act_norm(j - 2)
             if valid(j + 1):
                 pe_var_transposes(j + 1)
                 pe_mean_copy(j + 1)
             if j == -1:
                 nc.tensor.matmul(w_ps[:], lhsT=ones_bf[:], rhs=wrow[:], start=True, stop=True)
                 nc.tensor.matmul(b_ps[:], lhsT=ones_bf[:], rhs=brow[:], start=True, stop=True)
-            if valid(j):
-                dve_noise(j)
+            if valid(j - 3):
+                dve_hat(j - 3, 0)
+                dve_hat(j - 3, 1)
+                pe_hat_transposes(j - 3)
             if valid(j - 4):
                 dve_quantise(j - 4)
             if is_x(j - 4):
                 pe_products(j - 4)
-            if valid(j - 1):
-                pool_rstd(j - 1)
-            if valid(j - 2):
-                act_norm(j - 2)
-                pool_rnorm(j - 2)
+            if valid(j - 1) or valid(j - 2):
+                roots(j - 1, j - 2)
             if valid(j + 1):
                 act_std(j + 1)
+                pool_noise(j + 1)
+            if 0 <= j - 2 < P_TILES:
+                column_rep(j - 2)
             if valid(j - 3):
                 act_regroup(j - 3)
             if valid(j):
                 dve_mean(j, 0)
                 dve_mean(j, 1)
-                pool_negmu(j)
-            if 0 <= j - 2 < P_TILES:
-                column_rep(j - 2)
-            if valid(j - 2):
-                pool_hat(j - 2, 0)
-                pool_hat(j - 2, 1)
-                pe_hat_transposes(j - 2)
             if valid(j - 1):
                 dve_gain(j - 1, 0)
                 dve_gain(j - 1, 1)
@@ -340,4 +342,5 @@ def tile_probprotoseghead_t_kernel(tc, x, x_var, prototypes, proto_var, eps_x, e
             if 0 <= j - 2 < P_TILES:
                 column_copy(j - 2)
             if valid(j):
+                act_negmu(j)
                 act_var(j)

@@ -30,7 +30,7 @@ def tile_probprotoseghead_t_kernel(tc, x, x_var, prototypes, proto_var, eps_x, e
     nc = tc.nc
     with ExitStack() as ctx:
         const = ctx.enter_context(tc.tile_pool(name="const", bufs=1))
-        io = ctx.enter_context(tc.tile_pool(name="io", bufs=3))
+        io = ctx.enter_context(tc.tile_pool(name="io", bufs=4))
         work = ctx.enter_context(tc.tile_pool(name="work", bufs=3))
         small = ctx.enter_context(tc.tile_pool(name="small", bufs=4))
         psc = ctx.enter_context(tc.psum_pool(name="psc", bufs=1))
@@ -75,14 +75,17 @@ def tile_probprotoseghead_t_kernel(tc, x, x_var, prototypes, proto_var, eps_x, e
             eps_t = io.tile([P, R, GROUP, K], BF16, name="eps_t", tag="eps_t")
             if g == 0:
                 srcs = (pvar_v, ep_v, p_v)
-                sl = slice(0, GROUP)
+                base = 0
             else:
                 srcs = (xvar_v, ex_v, x_v)
-                sl = slice((g - 1) * GROUP, g * GROUP)
-            nc.sync.dma_start(out=var_t[:], in_=srcs[0][:, sl, :])
-            for r in range(R):
-                nc.sync.dma_start(out=eps_t[:, r], in_=srcs[1][r][:, sl, :])
-            nc.sync.dma_start(out=mean_t[:], in_=srcs[2][:, sl, :])
+                base = (g - 1) * GROUP
+            cuts = [(0, 1), (1, GROUP)] if g == 0 else [(0, GROUP)]
+            for lo, hi in cuts:
+                part = slice(base + lo, base + hi)
+                nc.sync.dma_start(out=var_t[:, lo:hi, :], in_=srcs[0][:, part, :])
+                for r in range(R):
+                    nc.sync.dma_start(out=eps_t[:, r, lo:hi, :], in_=srcs[1][r][:, part, :])
+                nc.sync.dma_start(out=mean_t[:, lo:hi, :], in_=srcs[2][:, part, :])
             groups[g] = (var_t, eps_t, mean_t)
 
         def valid(i):
@@ -102,12 +105,12 @@ def tile_probprotoseghead_t_kernel(tc, x, x_var, prototypes, proto_var, eps_x, e
         def act_std(i):
             d = st[i]
             var_t = groups[i // GROUP][0]
-            s = work.tile([P, K], F32, name="s", tag="s")
+            s = work.tile([P, K], F32, name="s", tag="s", bufs=4)
             nc.scalar.activation(out=s[:], in_=var_t[:, i % GROUP, :], func=ACT.Exp, scale=0.5)
             junk = work.tile([P, K], BF16, name="junk", tag="junk", bufs=2)
-            svar = small.tile([P, 1], F32, name="svar", tag="svar", bufs=8)
+            svar = small.tile([P, 1], F32, name="svar", tag="svar", bufs=10)
             nc.scalar.activation(out=junk[:], in_=var_t[:, i % GROUP, :], func=ACT.Exp, accum_out=svar[:])
-            gs = work.tile([P, K], BF16, name="gs", tag="gs", bufs=7, align_bytes=64)
+            gs = work.tile([P, K], BF16, name="gs", tag="gs", bufs=9, align_bytes=64)
             nc.scalar.activation(
                 out=gs[:].rearrange("p (n u e) -> p n u e", u=2, e=2),
                 in_=d["ts"][:].bitcast(BF16).rearrange("p (u n e) -> p n u e", u=2, e=2),
@@ -141,19 +144,13 @@ def tile_probprotoseghead_t_kernel(tc, x, x_var, prototypes, proto_var, eps_x, e
                 op0=ALU.mult, op1=ALU.add, accum_out=d["sv"][:, r:r + 1],
             )
 
-        def act_negmu(i):
-            d = st[i]
-            negmu = small.tile([P, R], F32, name="negmu", tag="negmu")
-            nc.scalar.mul(out=negmu[:], in_=d["sv"][:], mul=-1.0 / K)
-            d["negmu"] = negmu
-
         def act_var(i):
             d = st[i]
             ssq = small.tile([P, R], F32, name="ssq", tag="ssq")
             for r in range(R):
                 junk = work.tile([P, K], BF16, name="junk", tag="junk", bufs=2)
                 nc.scalar.activation(
-                    out=junk[:], in_=d["v"][:, r, :], func=ACT.Square, bias=d["negmu"][:, r:r + 1], scale=1.0,
+                    out=junk[:], in_=d["v"][:, r, :], func=ACT.Square, bias=d["sv"][:, r:r + 1], scale=-1.0 * K,
                     accum_out=ssq[:, r:r + 1],
                 )
             d["ssq"] = ssq
@@ -168,8 +165,11 @@ def tile_probprotoseghead_t_kernel(tc, x, x_var, prototypes, proto_var, eps_x, e
                     op0=ALU.mult, op1=ALU.add,
                 )
                 d["rowc"] = rowc
+                negmu = small.tile([P, R], F32, name="negmu", tag="negmu")
+                nc.vector.tensor_scalar(out=negmu[:], in0=d["sv"][:], scalar1=-1.0 / K, scalar2=None, op0=ALU.mult)
+                d["negmu"] = negmu
                 nc.vector.tensor_scalar(
-                    out=pin[:, 0:R], in0=d["ssq"][:], scalar1=1.0 / K, scalar2=LN_EPS, op0=ALU.mult, op1=ALU.add
+                    out=pin[:, 0:R], in0=d["ssq"][:], scalar1=1.0 / (K * K * K), scalar2=LN_EPS, op0=ALU.mult, op1=ALU.add
                 )
             else:
                 nc.vector.memset(pin[:, 0:R], 1.0)
@@ -221,11 +221,12 @@ def tile_probprotoseghead_t_kernel(tc, x, x_var, prototypes, proto_var, eps_x, e
 
         def pe_hat_transposes(i):
             d = st[i]
-            tx = psw.tile([P, R, 4, P], BF16, name="tx", tag="tx")
+            d["tx"] = []
             for r in range(R):
+                tx = psc.tile([P, 4, P], BF16, name="tx%d" % r, tag="tx%d" % r)
                 for q in range(4):
-                    nc.tensor.transpose(tx[:, r, q, :], d["xh"][:, r, q * P:(q + 1) * P], ident_bf[:])
-            d["tx"] = tx
+                    nc.tensor.transpose(tx[:, q, :], d["xh"][:, r, q * P:(q + 1) * P], ident_bf[:])
+                d["tx"].append(tx)
 
         def column_rep(i):
             d = st[i]
@@ -238,11 +239,20 @@ def tile_probprotoseghead_t_kernel(tc, x, x_var, prototypes, proto_var, eps_x, e
         def column_copy(i):
             nc.vector.tensor_copy(out=col_term[:, i * P:(i + 1) * P], in_=st[i]["tc_ps"][:, 0:P])
 
+        def vector_share(i):
+            return i % 3 == 2
+
         def act_regroup(i):
             d = st[i]
             gx = work.tile([P, R, P, 4], BF16, name="gx", tag="gx", align_bytes=64)
-            nc.scalar.copy(out=gx[:], in_=d["tx"][:].rearrange("p r q n -> p r n q"))
             d["gx"] = gx
+            for r in range(R):
+                if r == 0 or not vector_share(i):
+                    nc.scalar.copy(out=gx[:, r], in_=d["tx"][r][:].rearrange("p q n -> p n q"))
+
+        def dve_regroup(i):
+            d = st[i]
+            nc.vector.tensor_copy(out=d["gx"][:, 1], in_=d["tx"][1][:].rearrange("p q n -> p n q"))
 
         def dve_quantise(i):
             d = st[i]
@@ -301,13 +311,14 @@ def tile_probprotoseghead_t_kernel(tc, x, x_var, prototypes, proto_var, eps_x, e
         nc.sync.dma_start(out=wrow[0:1, :], in_=ln_w.unsqueeze(0))
         nc.sync.dma_start(out=brow[0:1, :], in_=ln_b.unsqueeze(0))
         load_group(1)
-        for j in range(-1, ITEMS + 4):
-            if valid(j + 1) and (j + 1) % GROUP == 0 and (j + 1) // GROUP + 2 < n_groups:
-                load_group((j + 1) // GROUP + 2)
+        for j in range(-3, ITEMS + 4):
+            if valid(j + 3) and (j + 3) % GROUP == 0 and (j + 3) // GROUP + 2 < n_groups:
+                load_group((j + 3) // GROUP + 2)
             if valid(j - 2):
                 act_norm(j - 2)
+            if valid(j + 3):
+                pe_var_transposes(j + 3)
             if valid(j + 1):
-                pe_var_transposes(j + 1)
                 pe_mean_copy(j + 1)
             if j == -1:
                 nc.tensor.matmul(w_ps[:], lhsT=ones_bf[:], rhs=wrow[:], start=True, stop=True)
@@ -322,8 +333,9 @@ def tile_probprotoseghead_t_kernel(tc, x, x_var, prototypes, proto_var, eps_x, e
                 pe_products(j - 4)
             if valid(j - 1) or valid(j - 2):
                 roots(j - 1, j - 2)
+            if valid(j + 3):
+                act_std(j + 3)
             if valid(j + 1):
-                act_std(j + 1)
                 pool_noise(j + 1)
             if 0 <= j - 2 < P_TILES:
                 column_rep(j - 2)
@@ -337,10 +349,11 @@ def tile_probprotoseghead_t_kernel(tc, x, x_var, prototypes, proto_var, eps_x, e
                 dve_gain(j - 1, 1)
                 dve_bias(j - 1, 0)
                 dve_bias(j - 1, 1)
+            if valid(j - 3) and vector_share(j - 3):
+                dve_regroup(j - 3)
             if is_x(j - 4):
                 dve_output(j - 4)
             if 0 <= j - 2 < P_TILES:
                 column_copy(j - 2)
             if valid(j):
-                act_negmu(j)
                 act_var(j)

@@ -21,7 +21,7 @@ X_TILES = N_ROWS // P
 P_TILES = CM // P
 ITEMS = P_TILES + X_TILES
 LN_EPS = 1e-5
-LAMDA = 1.0 / 128.0
+LN_LAMDA = -4.852030263919617
 
 FLOPS = 2 * (R * N_ROWS) * (R * CM) * K + 2 * N_ROWS * CM * K
 
@@ -51,8 +51,8 @@ def tile_probprotoseghead_t_kernel(tc, x, x_var, prototypes, proto_var, eps_x, e
         nc.vector.memset(brow[:], 0.0)
         ones_bf = const.tile([P, P], BF16, name="ones_bf")
         nc.vector.memset(ones_bf[:], 1.0)
-        ones_f = const.tile([P, P], F32, name="ones_f")
-        nc.vector.memset(ones_f[:], 1.0)
+        zero_f = const.tile([P, P], F32, name="zero_f")
+        nc.vector.memset(zero_f[:], 0.0)
         mhalf = const.tile([P, 2 * R], F32, name="mhalf")
         nc.vector.memset(mhalf[:], -0.5)
         ident_bf = const.tile([P, P], BF16, name="ident_bf")
@@ -108,8 +108,8 @@ def tile_probprotoseghead_t_kernel(tc, x, x_var, prototypes, proto_var, eps_x, e
             s = work.tile([P, K], F32, name="s", tag="s", bufs=4)
             nc.scalar.activation(out=s[:], in_=var_t[:, i % GROUP, :], func=ACT.Exp, scale=0.5)
             junk = work.tile([P, K], BF16, name="junk", tag="junk", bufs=2)
-            svar = small.tile([P, 1], F32, name="svar", tag="svar", bufs=10)
-            nc.scalar.activation(out=junk[:], in_=var_t[:, i % GROUP, :], func=ACT.Exp, accum_out=svar[:])
+            svar = small.tile([P, 1], F32, name="svar", tag="svar", bufs=12)
+            nc.scalar.activation(out=junk[:], in_=var_t[:, i % GROUP, :], func=ACT.Exp, bias=LN_LAMDA, accum_out=svar[:])
             gs = work.tile([P, K], BF16, name="gs", tag="gs", bufs=9, align_bytes=64)
             nc.scalar.activation(
                 out=gs[:].rearrange("p (n u e) -> p n u e", u=2, e=2),
@@ -131,7 +131,8 @@ def tile_probprotoseghead_t_kernel(tc, x, x_var, prototypes, proto_var, eps_x, e
             d = st[i]
             eps_t = groups[i // GROUP][1]
             v = work.tile([P, R, K], F32, name="v", tag="v", bufs=4)
-            nc.gpsimd.tensor_tensor(
+            engine = nc.vector if i < 2 else nc.gpsimd
+            engine.tensor_tensor(
                 out=v[:], in0=eps_t[:, :, i % GROUP, :], in1=d["s"][:].unsqueeze(1).to_broadcast([P, R, K]), op=ALU.mult
             )
             d["v"] = v
@@ -159,12 +160,6 @@ def tile_probprotoseghead_t_kernel(tc, x, x_var, prototypes, proto_var, eps_x, e
             pin = small.tile([P, 2 * R], F32, name="pin", tag="pin")
             if valid(i_var):
                 d = st[i_var]
-                rowc = small.tile([P, 1], F32, name="rowc", tag="rowc", bufs=8)
-                nc.vector.tensor_scalar(
-                    out=rowc[:], in0=d["svar"][:], scalar1=-LAMDA, scalar2=(-2.0 if i_var < P_TILES else 0.0),
-                    op0=ALU.mult, op1=ALU.add,
-                )
-                d["rowc"] = rowc
                 negmu = small.tile([P, R], F32, name="negmu", tag="negmu")
                 nc.vector.tensor_scalar(out=negmu[:], in0=d["sv"][:], scalar1=-1.0 / K, scalar2=None, op0=ALU.mult)
                 d["negmu"] = negmu
@@ -231,7 +226,7 @@ def tile_probprotoseghead_t_kernel(tc, x, x_var, prototypes, proto_var, eps_x, e
         def column_rep(i):
             d = st[i]
             crep = work.tile([P, P], F32, name="crep", tag="crep", bufs=2)
-            nc.vector.tensor_scalar(out=crep[:], in0=ones_f[:], scalar1=d["rowc"][:], scalar2=None, op0=ALU.mult)
+            nc.vector.tensor_scalar(out=crep[:], in0=zero_f[:], scalar1=d["svar"][:], scalar2=-2.0, op0=ALU.subtract, op1=ALU.add)
             tc_ps = psc.tile([P, K // 2], F32, name="tc_ps", tag="ts")
             nc.tensor.transpose(tc_ps[:, 0:P], crep[:], ident_f[:])
             d["tc_ps"] = tc_ps
@@ -239,20 +234,12 @@ def tile_probprotoseghead_t_kernel(tc, x, x_var, prototypes, proto_var, eps_x, e
         def column_copy(i):
             nc.vector.tensor_copy(out=col_term[:, i * P:(i + 1) * P], in_=st[i]["tc_ps"][:, 0:P])
 
-        def vector_share(i):
-            return i % 3 == 2
-
         def act_regroup(i):
             d = st[i]
             gx = work.tile([P, R, P, 4], BF16, name="gx", tag="gx", align_bytes=64)
             d["gx"] = gx
             for r in range(R):
-                if r == 0 or not vector_share(i):
-                    nc.scalar.copy(out=gx[:, r], in_=d["tx"][r][:].rearrange("p q n -> p n q"))
-
-        def dve_regroup(i):
-            d = st[i]
-            nc.vector.tensor_copy(out=d["gx"][:, 1], in_=d["tx"][1][:].rearrange("p q n -> p n q"))
+                nc.scalar.copy(out=gx[:, r], in_=d["tx"][r][:].rearrange("p q n -> p n q"))
 
         def dve_quantise(i):
             d = st[i]
@@ -301,7 +288,7 @@ def tile_probprotoseghead_t_kernel(tc, x, x_var, prototypes, proto_var, eps_x, e
                 st["o"] = work.tile([P, 2, CM], F32, name="o", tag="o")
             o = st["o"]
             nc.vector.scalar_tensor_tensor(
-                out=o[:, t % 2, :], in0=d["acc"][:], scalar=d["rowc"][:], in1=col_term[:], op0=ALU.add, op1=ALU.add
+                out=o[:, t % 2, :], in0=d["acc"][:], scalar=d["svar"][:], in1=col_term[:], op0=ALU.subtract, op1=ALU.add
             )
             if t % 2 == 1:
                 nc.sync.dma_start(out=out_v[:, t - 1:t + 1, :], in_=o[:])
@@ -349,8 +336,6 @@ def tile_probprotoseghead_t_kernel(tc, x, x_var, prototypes, proto_var, eps_x, e
                 dve_gain(j - 1, 1)
                 dve_bias(j - 1, 0)
                 dve_bias(j - 1, 1)
-            if valid(j - 3) and vector_share(j - 3):
-                dve_regroup(j - 3)
             if is_x(j - 4):
                 dve_output(j - 4)
             if 0 <= j - 2 < P_TILES:

@@ -35,7 +35,6 @@ def tile_probprotoseghead_t_kernel(tc, x, x_var, prototypes, proto_var, eps_x, e
         small = ctx.enter_context(tc.tile_pool(name="small", bufs=4))
         psc = ctx.enter_context(tc.psum_pool(name="psc", bufs=1))
         psw = ctx.enter_context(tc.psum_pool(name="psw", bufs=2))
-        ctx.enter_context(tc.manual_schedule())
 
         x_v = x.rearrange("(p t) k -> p t k", t=X_TILES)
         xvar_v = x_var.rearrange("(p t) k -> p t k", t=X_TILES)

@@ -35,6 +35,7 @@ def tile_probprotoseghead_t_kernel(tc, x, x_var, prototypes, proto_var, eps_x, e
         small = ctx.enter_context(tc.tile_pool(name="small", bufs=4))
         psc = ctx.enter_context(tc.psum_pool(name="psc", bufs=1))
         psw = ctx.enter_context(tc.psum_pool(name="psw", bufs=2))
+        ctx.enter_context(tc.manual_schedule())
 
         x_v = x.rearrange("(p t) k -> p t k", t=X_TILES)
         xvar_v = x_var.rearrange("(p t) k -> p t k", t=X_TILES)
@@ -215,12 +216,11 @@ def tile_probprotoseghead_t_kernel(tc, x, x_var, prototypes, proto_var, eps_x, e
 
         def pe_hat_transposes(i):
             d = st[i]
-            d["tx"] = []
+            tx = psc.tile([P, R, 4, P], BF16, name="tx", tag="tx")
             for r in range(R):
-                tx = psc.tile([P, 4, P], BF16, name="tx%d" % r, tag="tx%d" % r)
                 for q in range(4):
-                    nc.tensor.transpose(tx[:, q, :], d["xh"][:, r, q * P:(q + 1) * P], ident_bf[:])
-                d["tx"].append(tx)
+                    nc.tensor.transpose(tx[:, r, q, :], d["xh"][:, r, q * P:(q + 1) * P], ident_bf[:])
+            d["tx"] = tx
 
         def column_rep(i):
             d = st[i]
@@ -237,8 +237,7 @@ def tile_probprotoseghead_t_kernel(tc, x, x_var, prototypes, proto_var, eps_x, e
             d = st[i]
             gx = work.tile([P, R, P, 4], BF16, name="gx", tag="gx", align_bytes=64)
             d["gx"] = gx
-            for r in range(R):
-                nc.scalar.copy(out=gx[:, r], in_=d["tx"][r][:].rearrange("p q n -> p n q"))
+            nc.scalar.copy(out=gx[:], in_=d["tx"][:].rearrange("p r q n -> p r n q"))
 
         def dve_quantise(i):
             d = st[i]
@@ -266,7 +265,7 @@ def tile_probprotoseghead_t_kernel(tc, x, x_var, prototypes, proto_var, eps_x, e
 
         def pe_products(i):
             d = st[i]
-            acc = psc.tile([P, CM], F32, name="acc", tag="acc")
+            acc = psw.tile([P, CM], F32, name="acc", tag="acc")
             passes = [(r, b) for r in range(R) for b in range(R)] + [(R, R)]
             for n, (a, b) in enumerate(passes):
                 nc.tensor.matmul_mx(
@@ -282,22 +281,18 @@ def tile_probprotoseghead_t_kernel(tc, x, x_var, prototypes, proto_var, eps_x, e
 
         def dve_output(i):
             d = st[i]
-            t = i - P_TILES
-            if t % 2 == 0:
-                st["o"] = work.tile([P, 2, CM], F32, name="o", tag="o")
-            o = st["o"]
+            o = work.tile([P, CM], F32, name="o", tag="o", bufs=4)
             nc.vector.scalar_tensor_tensor(
-                out=o[:, t % 2, :], in0=d["acc"][:], scalar=d["svar"][:], in1=col_term[:], op0=ALU.subtract, op1=ALU.add
+                out=o[:], in0=d["acc"][:], scalar=d["svar"][:], in1=col_term[:], op0=ALU.subtract, op1=ALU.add
             )
-            if t % 2 == 1:
-                nc.sync.dma_start(out=out_v[:, t - 1:t + 1, :], in_=o[:])
+            nc.sync.dma_start(out=out_v[:, i - P_TILES, :], in_=o[:])
 
         n_groups = ITEMS // GROUP
         load_group(0)
         nc.sync.dma_start(out=wrow[0:1, :], in_=ln_w.unsqueeze(0))
         nc.sync.dma_start(out=brow[0:1, :], in_=ln_b.unsqueeze(0))
         load_group(1)
-        for j in range(-3, ITEMS + 4):
+        for j in range(-3, ITEMS + 5):
             if valid(j + 3) and (j + 3) % GROUP == 0 and (j + 3) // GROUP + 2 < n_groups:
                 load_group((j + 3) // GROUP + 2)
             if valid(j - 2):
@@ -335,8 +330,8 @@ def tile_probprotoseghead_t_kernel(tc, x, x_var, prototypes, proto_var, eps_x, e
                 dve_gain(j - 1, 1)
                 dve_bias(j - 1, 0)
                 dve_bias(j - 1, 1)
-            if is_x(j - 4):
-                dve_output(j - 4)
+            if is_x(j - 5):
+                dve_output(j - 5)
             if 0 <= j - 2 < P_TILES:
                 column_copy(j - 2)
             if valid(j):

@@ -16,14 +16,31 @@ K = 512
 N_ROWS = 4096
 CM = 512
 R = 2
+CHUNKS = K // P
 GROUP = 4
-X_TILES = N_ROWS // P
-P_TILES = CM // P
-ITEMS = P_TILES + X_TILES
+P_ITEMS = CM // P
+X_ITEMS = N_ROWS // P
+ITEMS = P_ITEMS + X_ITEMS
+N_GROUPS = ITEMS // GROUP
 LN_EPS = 1e-5
 LN_LAMDA = -4.852030263919617
+VECTOR_NOISE_ITEMS = 2
+
+EXPS = -3
+NOISE = -1
+MEAN = 0
+AFFINE = 1
+NORM = 2
+ROOT = 3
+HAT = 4
+QUANT = 5
+OUT = 6
 
 FLOPS = 2 * (R * N_ROWS) * (R * CM) * K + 2 * N_ROWS * CM * K
+
+
+def depth(first, last):
+    return last - first + 2
 
 
 def tile_probprotoseghead_t_kernel(tc, x, x_var, prototypes, proto_var, eps_x, eps_p, ln_w, ln_b, out):
@@ -31,308 +48,328 @@ def tile_probprotoseghead_t_kernel(tc, x, x_var, prototypes, proto_var, eps_x, e
     with ExitStack() as ctx:
         const = ctx.enter_context(tc.tile_pool(name="const", bufs=1))
         io = ctx.enter_context(tc.tile_pool(name="io", bufs=4))
-        work = ctx.enter_context(tc.tile_pool(name="work", bufs=3))
-        small = ctx.enter_context(tc.tile_pool(name="small", bufs=4))
-        psc = ctx.enter_context(tc.psum_pool(name="psc", bufs=1))
-        psw = ctx.enter_context(tc.psum_pool(name="psw", bufs=2))
+        work = ctx.enter_context(tc.tile_pool(name="work", bufs=2))
+        small = ctx.enter_context(tc.tile_pool(name="small", bufs=2))
+        psum_one = ctx.enter_context(tc.psum_pool(name="psum_one", bufs=1))
+        psum_two = ctx.enter_context(tc.psum_pool(name="psum_two", bufs=2))
         ctx.enter_context(tc.manual_schedule())
 
-        x_v = x.rearrange("(p t) k -> p t k", t=X_TILES)
-        xvar_v = x_var.rearrange("(p t) k -> p t k", t=X_TILES)
-        ex_v = [eps_x[r].rearrange("(p t) k -> p t k", t=X_TILES) for r in range(R)]
-        out_v = out.rearrange("(p t) c m -> p t (c m)", t=X_TILES)
-        p_v = prototypes.rearrange("(j c) m k -> (c m) j k", j=P_TILES)
-        pvar_v = proto_var.rearrange("(j c) m k -> (c m) j k", j=P_TILES)
-        ep_v = [eps_p[r].rearrange("(j c) m k -> (c m) j k", j=P_TILES) for r in range(R)]
+        x_v = x.rearrange("(p t) k -> p t k", t=X_ITEMS)
+        xvar_v = x_var.rearrange("(p t) k -> p t k", t=X_ITEMS)
+        ex_v = [eps_x[r].rearrange("(p t) k -> p t k", t=X_ITEMS) for r in range(R)]
+        out_v = out.rearrange("(p t) c m -> p t (c m)", t=X_ITEMS)
+        p_v = prototypes.rearrange("(j c) m k -> (c m) j k", j=P_ITEMS)
+        pvar_v = proto_var.rearrange("(j c) m k -> (c m) j k", j=P_ITEMS)
+        ep_v = [eps_p[r].rearrange("(j c) m k -> (c m) j k", j=P_ITEMS) for r in range(R)]
 
-        wrow = const.tile([P, K], BF16, name="wrow")
-        brow = const.tile([P, K], BF16, name="brow")
-        nc.vector.memset(wrow[:], 0.0)
-        nc.vector.memset(brow[:], 0.0)
+        w_row = const.tile([P, K], BF16, name="w_row")
+        b_row = const.tile([P, K], BF16, name="b_row")
+        nc.vector.memset(w_row[:], 0.0)
+        nc.vector.memset(b_row[:], 0.0)
         ones_bf = const.tile([P, P], BF16, name="ones_bf")
         nc.vector.memset(ones_bf[:], 1.0)
         zero_f = const.tile([P, P], F32, name="zero_f")
         nc.vector.memset(zero_f[:], 0.0)
-        mhalf = const.tile([P, 2 * R], F32, name="mhalf")
-        nc.vector.memset(mhalf[:], -0.5)
+        minus_half = const.tile([P, 2 * R], F32, name="minus_half")
+        nc.vector.memset(minus_half[:], -0.5)
         ident_bf = const.tile([P, P], BF16, name="ident_bf")
         make_identity(nc, ident_bf[:])
         ident_f = const.tile([P, P], F32, name="ident_f")
         make_identity(nc, ident_f[:])
-        w_ps = psc.tile([P, K], F32, name="w_ps")
-        b_ps = psc.tile([P, K], F32, name="b_ps")
+        w_ps = psum_one.tile([P, K], F32, name="w_ps")
+        b_ps = psum_one.tile([P, K], F32, name="b_ps")
 
         col_term = const.tile([P, CM], F32, name="col_term")
         p_codes = const.tile([P, R + 1, CM], U32, name="p_codes", align_bytes=64)
         p_scales = const.tile([P, R + 1, CM], U8, name="p_scales", align_bytes=64)
 
         groups = {}
-        st = {}
+        state = {}
+
+        def valid(i):
+            return 0 <= i < ITEMS
+
+        def is_prototype(i):
+            return 0 <= i < P_ITEMS
+
+        def is_feature(i):
+            return P_ITEMS <= i < ITEMS
 
         def load_group(g):
             var_t = io.tile([P, GROUP, K], BF16, name="var_t", tag="var_t")
             mean_t = io.tile([P, GROUP, K], BF16, name="mean_t", tag="mean_t")
             eps_t = io.tile([P, R, GROUP, K], BF16, name="eps_t", tag="eps_t")
             if g == 0:
-                srcs = (pvar_v, ep_v, p_v)
-                base = 0
+                var_v, eps_v, mean_v, first = pvar_v, ep_v, p_v, 0
+                cuts = [(0, 1), (1, GROUP)]
             else:
-                srcs = (xvar_v, ex_v, x_v)
-                base = (g - 1) * GROUP
-            cuts = [(0, 1), (1, GROUP)] if g == 0 else [(0, GROUP)]
+                var_v, eps_v, mean_v, first = xvar_v, ex_v, x_v, (g - 1) * GROUP
+                cuts = [(0, GROUP)]
             for lo, hi in cuts:
-                part = slice(base + lo, base + hi)
-                nc.sync.dma_start(out=var_t[:, lo:hi, :], in_=srcs[0][:, part, :])
+                part = slice(first + lo, first + hi)
+                nc.sync.dma_start(out=var_t[:, lo:hi, :], in_=var_v[:, part, :])
                 for r in range(R):
-                    nc.sync.dma_start(out=eps_t[:, r, lo:hi, :], in_=srcs[1][r][:, part, :])
-                nc.sync.dma_start(out=mean_t[:, lo:hi, :], in_=srcs[2][:, part, :])
-            groups[g] = (var_t, eps_t, mean_t)
+                    nc.sync.dma_start(out=eps_t[:, r, lo:hi, :], in_=eps_v[r][:, part, :])
+                nc.sync.dma_start(out=mean_t[:, lo:hi, :], in_=mean_v[:, part, :])
+            groups[g] = {"var": var_t, "eps": eps_t, "mean": mean_t}
 
-        def valid(i):
-            return 0 <= i < ITEMS
+        def inputs(i, name):
+            return groups[i // GROUP][name]
 
-        def is_x(i):
-            return P_TILES <= i < ITEMS
+        def broadcast_gain_and_bias():
+            nc.tensor.matmul(w_ps[:], lhsT=ones_bf[:], rhs=w_row[:], start=True, stop=True)
+            nc.tensor.matmul(b_ps[:], lhsT=ones_bf[:], rhs=b_row[:], start=True, stop=True)
 
-        def pe_var_transposes(i):
-            var_t = groups[i // GROUP][0]
-            words = var_t[:, i % GROUP, :].bitcast(F32)
-            ts = psc.tile([P, K // 2], F32, name="ts", tag="ts")
-            for u in range(2):
-                nc.tensor.transpose(ts[:, u * P:(u + 1) * P], words[:, u * P:(u + 1) * P], ident_f[:])
-            st[i] = {"ts": ts}
+        def transpose_log_variance(i):
+            words = inputs(i, "var")[:, i % GROUP, :].bitcast(F32)
+            var_ps = psum_one.tile([P, K // 2], F32, name="var_ps", tag="var_ps")
+            for h in range(2):
+                nc.tensor.transpose(var_ps[:, h * P:(h + 1) * P], words[:, h * P:(h + 1) * P], ident_f[:])
+            state[i] = {"var_ps": var_ps}
 
-        def act_std(i):
-            d = st[i]
-            var_t = groups[i // GROUP][0]
-            s = work.tile([P, K], F32, name="s", tag="s", bufs=4)
-            nc.scalar.activation(out=s[:], in_=var_t[:, i % GROUP, :], func=ACT.Exp, scale=0.5)
-            junk = work.tile([P, K], BF16, name="junk", tag="junk", bufs=2)
-            svar = small.tile([P, 1], F32, name="svar", tag="svar", bufs=12)
-            nc.scalar.activation(out=junk[:], in_=var_t[:, i % GROUP, :], func=ACT.Exp, bias=LN_LAMDA, accum_out=svar[:])
-            gs = work.tile([P, K], BF16, name="gs", tag="gs", bufs=9, align_bytes=64)
+        def exps(i):
+            d = state[i]
+            log_var = inputs(i, "var")[:, i % GROUP, :]
+            std = work.tile([P, K], F32, name="std", tag="std", bufs=depth(EXPS, NOISE))
+            nc.scalar.activation(out=std[:], in_=log_var, func=ACT.Exp, scale=0.5)
+            unused = work.tile([P, K], BF16, name="unused", tag="unused")
+            var_sum = small.tile([P, 1], F32, name="var_sum", tag="var_sum", bufs=depth(EXPS, OUT))
+            nc.scalar.activation(out=unused[:], in_=log_var, func=ACT.Exp, bias=LN_LAMDA, accum_out=var_sum[:])
+            std_grouped = work.tile(
+                [P, K], BF16, name="std_grouped", tag="std_grouped", bufs=depth(EXPS, QUANT), align_bytes=64
+            )
             nc.scalar.activation(
-                out=gs[:].rearrange("p (n u e) -> p n u e", u=2, e=2),
-                in_=d["ts"][:].bitcast(BF16).rearrange("p (u n e) -> p n u e", u=2, e=2),
+                out=std_grouped[:].rearrange("p (n h e) -> p n h e", h=2, e=2),
+                in_=d["var_ps"][:].bitcast(BF16).rearrange("p (h n e) -> p n h e", h=2, e=2),
                 func=ACT.Exp,
                 scale=0.5,
             )
-            d["s"] = s
-            d["svar"] = svar
-            d["gs"] = gs
+            d["std"] = std
+            d["var_sum"] = var_sum
+            d["std_grouped"] = std_grouped
 
-        def pe_mean_copy(i):
-            mean_t = groups[i // GROUP][2]
-            xps = psw.tile([P, K], F32, name="xps", tag="xps")
-            nc.tensor.matmul(xps[:], lhsT=ident_bf[:], rhs=mean_t[:, i % GROUP, :], start=True, stop=True)
-            st[i]["xps"] = xps
+        def copy_mean_to_psum(i):
+            mean_ps = psum_two.tile([P, K], F32, name="mean_ps", tag="mean_ps")
+            nc.tensor.matmul(mean_ps[:], lhsT=ident_bf[:], rhs=inputs(i, "mean")[:, i % GROUP, :], start=True, stop=True)
+            state[i]["mean_ps"] = mean_ps
 
-        def pool_noise(i):
-            d = st[i]
-            eps_t = groups[i // GROUP][1]
-            v = work.tile([P, R, K], F32, name="v", tag="v", bufs=4)
-            engine = nc.vector if i < 2 else nc.gpsimd
+        def noise(i):
+            d = state[i]
+            v = work.tile([P, R, K], F32, name="v", tag="v", bufs=depth(NOISE, AFFINE))
+            engine = nc.vector if i < VECTOR_NOISE_ITEMS else nc.gpsimd
             engine.tensor_tensor(
-                out=v[:], in0=eps_t[:, :, i % GROUP, :], in1=d["s"][:].unsqueeze(1).to_broadcast([P, R, K]), op=ALU.mult
+                out=v[:],
+                in0=inputs(i, "eps")[:, :, i % GROUP, :],
+                in1=d["std"][:].unsqueeze(1).to_broadcast([P, R, K]),
+                op=ALU.mult,
             )
             d["v"] = v
-            d["sv"] = small.tile([P, R], F32, name="sv", tag="sv")
+            d["row_sum"] = small.tile([P, R], F32, name="row_sum", tag="row_sum", bufs=depth(MEAN, AFFINE))
 
-        def dve_mean(i, r):
-            d = st[i]
+        def add_mean(i, r):
+            d = state[i]
             nc.vector.scalar_tensor_tensor(
-                out=d["v"][:, r, :], in0=d["v"][:, r, :], scalar=1.0, in1=d["xps"][:],
-                op0=ALU.mult, op1=ALU.add, accum_out=d["sv"][:, r:r + 1],
+                out=d["v"][:, r, :], in0=d["v"][:, r, :], scalar=1.0, in1=d["mean_ps"][:],
+                op0=ALU.mult, op1=ALU.add, accum_out=d["row_sum"][:, r:r + 1],
             )
 
-        def act_var(i):
-            d = st[i]
-            ssq = small.tile([P, R], F32, name="ssq", tag="ssq")
+        def squared_deviations(i):
+            d = state[i]
+            dev_sum = small.tile([P, R], F32, name="dev_sum", tag="dev_sum", bufs=depth(MEAN, AFFINE))
             for r in range(R):
-                junk = work.tile([P, K], BF16, name="junk", tag="junk", bufs=2)
+                unused = work.tile([P, K], BF16, name="unused", tag="unused")
                 nc.scalar.activation(
-                    out=junk[:], in_=d["v"][:, r, :], func=ACT.Square, bias=d["sv"][:, r:r + 1], scale=-1.0 * K,
-                    accum_out=ssq[:, r:r + 1],
+                    out=unused[:], in_=d["v"][:, r, :], func=ACT.Square, bias=d["row_sum"][:, r:r + 1], scale=-1.0 * K,
+                    accum_out=dev_sum[:, r:r + 1],
                 )
-            d["ssq"] = ssq
+            d["dev_sum"] = dev_sum
 
         def roots(i_var, i_norm):
-            pin = small.tile([P, 2 * R], F32, name="pin", tag="pin")
+            base = small.tile([P, 2 * R], F32, name="base", tag="base")
             if valid(i_var):
-                d = st[i_var]
-                negmu = small.tile([P, R], F32, name="negmu", tag="negmu")
-                nc.vector.tensor_scalar(out=negmu[:], in0=d["sv"][:], scalar1=-1.0 / K, scalar2=None, op0=ALU.mult)
-                d["negmu"] = negmu
+                d = state[i_var]
+                neg_mean = small.tile([P, R], F32, name="neg_mean", tag="neg_mean")
+                nc.vector.tensor_scalar(out=neg_mean[:], in0=d["row_sum"][:], scalar1=-1.0 / K, scalar2=None, op0=ALU.mult)
+                d["neg_mean"] = neg_mean
                 nc.vector.tensor_scalar(
-                    out=pin[:, 0:R], in0=d["ssq"][:], scalar1=1.0 / (K * K * K), scalar2=LN_EPS, op0=ALU.mult, op1=ALU.add
+                    out=base[:, 0:R], in0=d["dev_sum"][:], scalar1=1.0 / (K * K * K), scalar2=LN_EPS,
+                    op0=ALU.mult, op1=ALU.add,
                 )
             else:
-                nc.vector.memset(pin[:, 0:R], 1.0)
+                nc.vector.memset(base[:, 0:R], 1.0)
             if valid(i_norm):
                 nc.vector.tensor_scalar(
-                    out=pin[:, R:2 * R], in0=st[i_norm]["su2"][:], scalar1=1e-24,
-                    scalar2=(4.0 if i_norm < P_TILES else 1.0), op0=ALU.max, op1=ALU.mult,
+                    out=base[:, R:2 * R], in0=state[i_norm]["square_sum"][:], scalar1=1e-24,
+                    scalar2=(4.0 if is_prototype(i_norm) else 1.0), op0=ALU.max, op1=ALU.mult,
                 )
             else:
-                nc.vector.memset(pin[:, R:2 * R], 1.0)
-            pout = small.tile([P, 2 * R], F32, name="pout", tag="pout", bufs=6)
-            nc.gpsimd.tensor_tensor(out=pout[:], in0=pin[:], in1=mhalf[:], op=ALU.pow)
+                nc.vector.memset(base[:, R:2 * R], 1.0)
+            inv_root = small.tile([P, 2 * R], F32, name="inv_root", tag="inv_root", bufs=depth(ROOT, HAT))
+            nc.gpsimd.tensor_tensor(out=inv_root[:], in0=base[:], in1=minus_half[:], op=ALU.pow)
             if valid(i_var):
-                st[i_var]["rstd"] = pout[:, 0:R]
+                state[i_var]["rstd"] = inv_root[:, 0:R]
             if valid(i_norm):
-                st[i_norm]["dn"] = pout[:, R:2 * R]
+                state[i_norm]["inv_norm"] = inv_root[:, R:2 * R]
 
-        def dve_gain(i, r):
-            d = st[i]
+        def centre_and_gain(i, r):
+            d = state[i]
             if r == 0:
-                d["u"] = work.tile([P, R, K], F32, name="u", tag="u", bufs=4)
+                d["u"] = work.tile([P, R, K], F32, name="u", tag="u", bufs=depth(AFFINE, HAT))
             nc.vector.scalar_tensor_tensor(
-                out=d["u"][:, r, :], in0=d["v"][:, r, :], scalar=d["negmu"][:, r:r + 1], in1=w_ps[:],
+                out=d["u"][:, r, :], in0=d["v"][:, r, :], scalar=d["neg_mean"][:, r:r + 1], in1=w_ps[:],
                 op0=ALU.add, op1=ALU.mult,
             )
 
-        def dve_bias(i, r):
-            d = st[i]
+        def scale_and_bias(i, r):
+            d = state[i]
             nc.vector.scalar_tensor_tensor(
                 out=d["u"][:, r, :], in0=d["u"][:, r, :], scalar=d["rstd"][:, r:r + 1], in1=b_ps[:],
                 op0=ALU.mult, op1=ALU.add,
             )
 
-        def act_norm(i):
-            d = st[i]
-            su2 = small.tile([P, R], F32, name="su2", tag="su2")
+        def square_sums(i):
+            d = state[i]
+            square_sum = small.tile([P, R], F32, name="square_sum", tag="square_sum", bufs=depth(NORM, ROOT))
             for r in range(R):
-                junk = work.tile([P, K], BF16, name="junk", tag="junk", bufs=2)
-                nc.scalar.activation(out=junk[:], in_=d["u"][:, r, :], func=ACT.Square, accum_out=su2[:, r:r + 1])
-            d["su2"] = su2
+                unused = work.tile([P, K], BF16, name="unused", tag="unused")
+                nc.scalar.activation(out=unused[:], in_=d["u"][:, r, :], func=ACT.Square, accum_out=square_sum[:, r:r + 1])
+            d["square_sum"] = square_sum
 
-        def dve_hat(i, r):
-            d = st[i]
-            if r == 0:
-                d["xh"] = work.tile([P, R, K], BF16, name="xh", tag="xh")
+        def column_term_rows(i):
+            repeated = work.tile([P, P], F32, name="repeated", tag="repeated")
             nc.vector.tensor_scalar(
-                out=d["xh"][:, r, :], in0=d["u"][:, r, :], scalar1=d["dn"][:, r:r + 1], scalar2=None, op0=ALU.mult
+                out=repeated[:], in0=zero_f[:], scalar1=state[i]["var_sum"][:], scalar2=-2.0,
+                op0=ALU.subtract, op1=ALU.add,
+            )
+            term_ps = psum_one.tile([P, K // 2], F32, name="term_ps", tag="var_ps")
+            nc.tensor.transpose(term_ps[:, 0:P], repeated[:], ident_f[:])
+            state[i]["term_ps"] = term_ps
+
+        def column_term_copy(i):
+            nc.vector.tensor_copy(out=col_term[:, i * P:(i + 1) * P], in_=state[i]["term_ps"][:, 0:P])
+
+        def normalise(i, r):
+            d = state[i]
+            if r == 0:
+                d["hat"] = work.tile([P, R, K], BF16, name="hat", tag="hat")
+            nc.vector.tensor_scalar(
+                out=d["hat"][:, r, :], in0=d["u"][:, r, :], scalar1=d["inv_norm"][:, r:r + 1], scalar2=None, op0=ALU.mult
             )
 
-        def pe_hat_transposes(i):
-            d = st[i]
-            tx = psc.tile([P, R, 4, P], BF16, name="tx", tag="tx")
+        def transpose_hat(i):
+            d = state[i]
+            hat_ps = psum_one.tile([P, R, CHUNKS, P], BF16, name="hat_ps", tag="hat_ps")
             for r in range(R):
-                for q in range(4):
-                    nc.tensor.transpose(tx[:, r, q, :], d["xh"][:, r, q * P:(q + 1) * P], ident_bf[:])
-            d["tx"] = tx
+                for q in range(CHUNKS):
+                    nc.tensor.transpose(hat_ps[:, r, q, :], d["hat"][:, r, q * P:(q + 1) * P], ident_bf[:])
+            d["hat_ps"] = hat_ps
 
-        def column_rep(i):
-            d = st[i]
-            crep = work.tile([P, P], F32, name="crep", tag="crep", bufs=2)
-            nc.vector.tensor_scalar(out=crep[:], in0=zero_f[:], scalar1=d["svar"][:], scalar2=-2.0, op0=ALU.subtract, op1=ALU.add)
-            tc_ps = psc.tile([P, K // 2], F32, name="tc_ps", tag="ts")
-            nc.tensor.transpose(tc_ps[:, 0:P], crep[:], ident_f[:])
-            d["tc_ps"] = tc_ps
+        def regroup_hat(i):
+            d = state[i]
+            hat_grouped = work.tile(
+                [P, R, P, CHUNKS], BF16, name="hat_grouped", tag="hat_grouped", bufs=depth(HAT, QUANT), align_bytes=64
+            )
+            nc.scalar.copy(out=hat_grouped[:], in_=d["hat_ps"][:].rearrange("p r q n -> p r n q"))
+            d["hat_grouped"] = hat_grouped
 
-        def column_copy(i):
-            nc.vector.tensor_copy(out=col_term[:, i * P:(i + 1) * P], in_=st[i]["tc_ps"][:, 0:P])
-
-        def act_regroup(i):
-            d = st[i]
-            gx = work.tile([P, R, P, 4], BF16, name="gx", tag="gx", align_bytes=64)
-            d["gx"] = gx
-            nc.scalar.copy(out=gx[:], in_=d["tx"][:].rearrange("p r q n -> p r n q"))
-
-        def dve_quantise(i):
-            d = st[i]
-            if i < P_TILES:
+        def quantise(i):
+            d = state[i]
+            if is_prototype(i):
                 cols = slice(i * P, (i + 1) * P)
-                nc.vector.tensor_scalar(out=d["gs"][:], in0=d["gs"][:], scalar1=2.0 ** -6, scalar2=None, op0=ALU.mult)
+                nc.vector.tensor_scalar(
+                    out=d["std_grouped"][:], in0=d["std_grouped"][:], scalar1=2.0 ** -6, scalar2=None, op0=ALU.mult
+                )
                 for r in range(R):
                     nc.vector.quantize_mx(
                         out=p_codes[:, r, cols].bitcast(FP8X4), scales=p_scales[:, r, cols],
-                        in_=d["gx"][:, r].rearrange("p n q -> p (n q)"),
+                        in_=d["hat_grouped"][:, r].rearrange("p n q -> p (n q)"),
                     )
-                nc.vector.quantize_mx(out=p_codes[:, R, cols].bitcast(FP8X4), scales=p_scales[:, R, cols], in_=d["gs"][:])
+                nc.vector.quantize_mx(
+                    out=p_codes[:, R, cols].bitcast(FP8X4), scales=p_scales[:, R, cols], in_=d["std_grouped"][:]
+                )
             else:
                 codes = work.tile([P, (R + 1) * P], U32, name="codes", tag="codes", align_bytes=64)
                 scales = work.tile([P, (R + 1) * P], U8, name="scales", tag="scales", align_bytes=64)
                 nc.vector.quantize_mx(
                     out=codes[:, 0:R * P].bitcast(FP8X4), scales=scales[:, 0:R * P],
-                    in_=d["gx"][:].rearrange("p r n q -> p (r n q)"),
+                    in_=d["hat_grouped"][:].rearrange("p r n q -> p (r n q)"),
                 )
                 nc.vector.quantize_mx(
-                    out=codes[:, R * P:(R + 1) * P].bitcast(FP8X4), scales=scales[:, R * P:(R + 1) * P], in_=d["gs"][:]
+                    out=codes[:, R * P:(R + 1) * P].bitcast(FP8X4), scales=scales[:, R * P:(R + 1) * P],
+                    in_=d["std_grouped"][:],
                 )
                 d["codes"] = codes
                 d["scales"] = scales
 
-        def pe_products(i):
-            d = st[i]
-            acc = psw.tile([P, CM], F32, name="acc", tag="acc")
+        def products(i):
+            d = state[i]
+            acc = psum_two.tile([P, CM], F32, name="acc", tag="acc")
             passes = [(r, b) for r in range(R) for b in range(R)] + [(R, R)]
-            for n, (a, b) in enumerate(passes):
+            for step, (a, b) in enumerate(passes):
                 nc.tensor.matmul_mx(
                     out=acc[:],
                     lhsT=d["codes"][:, a * P:(a + 1) * P].bitcast(FP8X4),
                     lhsT_scale=d["scales"][:, a * P:(a + 1) * P],
                     rhs=p_codes[:, b, :].bitcast(FP8X4),
                     rhs_scale=p_scales[:, b, :],
-                    start=(n == 0),
-                    stop=(n == len(passes) - 1),
+                    start=(step == 0),
+                    stop=(step == len(passes) - 1),
                 )
             d["acc"] = acc
 
-        def dve_output(i):
-            d = st[i]
-            o = work.tile([P, CM], F32, name="o", tag="o", bufs=4)
+        def output(i):
+            d = state[i]
+            result = work.tile([P, CM], F32, name="result", tag="result", bufs=depth(OUT, OUT + 1))
             nc.vector.scalar_tensor_tensor(
-                out=o[:], in0=d["acc"][:], scalar=d["svar"][:], in1=col_term[:], op0=ALU.subtract, op1=ALU.add
+                out=result[:], in0=d["acc"][:], scalar=d["var_sum"][:], in1=col_term[:], op0=ALU.subtract, op1=ALU.add
             )
-            nc.sync.dma_start(out=out_v[:, i - P_TILES, :], in_=o[:])
+            nc.sync.dma_start(out=out_v[:, i - P_ITEMS, :], in_=result[:])
 
-        n_groups = ITEMS // GROUP
         load_group(0)
-        nc.sync.dma_start(out=wrow[0:1, :], in_=ln_w.unsqueeze(0))
-        nc.sync.dma_start(out=brow[0:1, :], in_=ln_b.unsqueeze(0))
+        nc.sync.dma_start(out=w_row[0:1, :], in_=ln_w.unsqueeze(0))
+        nc.sync.dma_start(out=b_row[0:1, :], in_=ln_b.unsqueeze(0))
         load_group(1)
-        for j in range(-3, ITEMS + 5):
-            if valid(j + 3) and (j + 3) % GROUP == 0 and (j + 3) // GROUP + 2 < n_groups:
-                load_group((j + 3) // GROUP + 2)
-            if valid(j - 2):
-                act_norm(j - 2)
-            if valid(j + 3):
-                pe_var_transposes(j + 3)
-            if valid(j + 1):
-                pe_mean_copy(j + 1)
-            if j == -1:
-                nc.tensor.matmul(w_ps[:], lhsT=ones_bf[:], rhs=wrow[:], start=True, stop=True)
-                nc.tensor.matmul(b_ps[:], lhsT=ones_bf[:], rhs=brow[:], start=True, stop=True)
-            if valid(j - 3):
-                dve_hat(j - 3, 0)
-                dve_hat(j - 3, 1)
-                pe_hat_transposes(j - 3)
-            if valid(j - 4):
-                dve_quantise(j - 4)
-            if is_x(j - 4):
-                pe_products(j - 4)
-            if valid(j - 1) or valid(j - 2):
-                roots(j - 1, j - 2)
-            if valid(j + 3):
-                act_std(j + 3)
-            if valid(j + 1):
-                pool_noise(j + 1)
-            if 0 <= j - 2 < P_TILES:
-                column_rep(j - 2)
-            if valid(j - 3):
-                act_regroup(j - 3)
-            if valid(j):
-                dve_mean(j, 0)
-                dve_mean(j, 1)
-            if valid(j - 1):
-                dve_gain(j - 1, 0)
-                dve_gain(j - 1, 1)
-                dve_bias(j - 1, 0)
-                dve_bias(j - 1, 1)
-            if is_x(j - 5):
-                dve_output(j - 5)
-            if 0 <= j - 2 < P_TILES:
-                column_copy(j - 2)
-            if valid(j):
-                act_var(j)
+        for j in range(EXPS, ITEMS + OUT):
+            i = j - EXPS
+            if valid(i) and i % GROUP == 0 and i // GROUP + 2 < N_GROUPS:
+                load_group(i // GROUP + 2)
+            if valid(j - EXPS):
+                transpose_log_variance(j - EXPS)
+            if valid(j - NOISE):
+                copy_mean_to_psum(j - NOISE)
+            if j == NOISE:
+                broadcast_gain_and_bias()
+            if valid(j - HAT):
+                normalise(j - HAT, 0)
+                normalise(j - HAT, 1)
+                transpose_hat(j - HAT)
+            if valid(j - QUANT):
+                quantise(j - QUANT)
+            if is_feature(j - QUANT):
+                products(j - QUANT)
+            if valid(j - AFFINE) or valid(j - ROOT):
+                roots(j - AFFINE, j - ROOT)
+            if valid(j - EXPS):
+                exps(j - EXPS)
+            if valid(j - NORM):
+                square_sums(j - NORM)
+            if valid(j - NOISE):
+                noise(j - NOISE)
+            if is_prototype(j - NORM):
+                column_term_rows(j - NORM)
+            if valid(j - HAT):
+                regroup_hat(j - HAT)
+            if valid(j - MEAN):
+                add_mean(j - MEAN, 0)
+                add_mean(j - MEAN, 1)
+            if valid(j - AFFINE):
+                centre_and_gain(j - AFFINE, 0)
+                centre_and_gain(j - AFFINE, 1)
+                scale_and_bias(j - AFFINE, 0)
+                scale_and_bias(j - AFFINE, 1)
+            if is_feature(j - OUT):
+                output(j - OUT)
+            if is_prototype(j - NORM):
+                column_term_copy(j - NORM)
+            if valid(j - MEAN):
+                squared_deviations(j - MEAN)

@@ -258,10 +258,11 @@ def tile_probprotoseghead_t_kernel(tc, x, x_var, prototypes, proto_var, eps_x, e
 
         def transpose_hat(i):
             d = state[i]
-            hat_ps = psum_one.tile([P, R, CHUNKS, P], BF16, name="hat_ps", tag="hat_ps")
+            hat_ps = psum_one.tile([P, R, 2, P], F32, name="hat_ps", tag="hat_ps")
             for r in range(R):
-                for q in range(CHUNKS):
-                    nc.tensor.transpose(hat_ps[:, r, q, :], d["hat"][:, r, q * P:(q + 1) * P], ident_bf[:])
+                words = d["hat"][:, r, :].bitcast(F32)
+                for h in range(2):
+                    nc.tensor.transpose(hat_ps[:, r, h, :], words[:, h * P:(h + 1) * P], ident_f[:])
             d["hat_ps"] = hat_ps
 
         def regroup_hat(i):
@@ -269,7 +270,10 @@ def tile_probprotoseghead_t_kernel(tc, x, x_var, prototypes, proto_var, eps_x, e
             hat_grouped = work.tile(
                 [P, R, P, CHUNKS], BF16, name="hat_grouped", tag="hat_grouped", bufs=depth(HAT, QUANT), align_bytes=64
             )
-            nc.scalar.copy(out=hat_grouped[:], in_=d["hat_ps"][:].rearrange("p r q n -> p r n q"))
+            nc.scalar.copy(
+                out=hat_grouped[:].rearrange("p r n q -> p r (n q)").bitcast(F32).rearrange("p r (n h) -> p r n h", h=2),
+                in_=d["hat_ps"][:].rearrange("p r h n -> p r n h"),
+            )
             d["hat_grouped"] = hat_grouped
 
         def quantise(i):

@@ -252,9 +252,13 @@ def tile_probprotoseghead_t_kernel(tc, x, x_var, prototypes, proto_var, eps_x, e
             d = state[i]
             if r == 0:
                 d["hat"] = work.tile([P, R, K], BF16, name="hat", tag="hat")
-            nc.vector.tensor_scalar(
-                out=d["hat"][:, r, :], in0=d["u"][:, r, :], scalar1=d["inv_norm"][:, r:r + 1], scalar2=None, op0=ALU.mult
-            )
+            if r == 0:
+                nc.scalar.activation(out=d["hat"][:, r, :], in_=d["u"][:, r, :], func=ACT.Copy, scale=d["inv_norm"][:, r:r + 1])
+            else:
+                nc.vector.tensor_scalar(
+                    out=d["hat"][:, r, :], in0=d["u"][:, r, :], scalar1=d["inv_norm"][:, r:r + 1], scalar2=None,
+                    op0=ALU.mult,
+                )
 
         def transpose_hat(i):
             d = state[i]

@@ -252,7 +252,7 @@ def tile_probprotoseghead_t_kernel(tc, x, x_var, prototypes, proto_var, eps_x, e
             d = state[i]
             if r == 0:
                 d["hat"] = work.tile([P, R, K], BF16, name="hat", tag="hat")
-            if r == 0:
+            if r == 0 and i % 3 != 2:
                 nc.scalar.activation(out=d["hat"][:, r, :], in_=d["u"][:, r, :], func=ACT.Copy, scale=d["inv_norm"][:, r:r + 1])
             else:
                 nc.vector.tensor_scalar(

@@ -24,6 +24,7 @@ ITEMS = P_ITEMS + X_ITEMS
 N_GROUPS = ITEMS // GROUP
 LN_EPS = 1e-5
 LN_LAMDA = -4.852030263919617
+SCALAR_TAIL_ITEMS = 7
 VECTOR_NOISE_ITEMS = 2
 
 EXPS = -3
@@ -252,7 +253,7 @@ def tile_probprotoseghead_t_kernel(tc, x, x_var, prototypes, proto_var, eps_x, e
             d = state[i]
             if r == 0:
                 d["hat"] = work.tile([P, R, K], BF16, name="hat", tag="hat")
-            if r == 0 and i % 3 != 2:
+            if i >= ITEMS - SCALAR_TAIL_ITEMS or (r == 0 and i % 3 != 2 and is_feature(i)):
                 nc.scalar.activation(out=d["hat"][:, r, :], in_=d["u"][:, r, :], func=ACT.Copy, scale=d["inv_norm"][:, r:r + 1])
             else:
                 nc.vector.tensor_scalar(

@@ -196,17 +196,14 @@ def tile_probprotoseghead_t_kernel(tc, x, x_var, prototypes, proto_var, eps_x, e
                     out=base[:, 0:R], in0=d["dev_sum"][:], scalar1=1.0 / (K * K * K), scalar2=LN_EPS,
                     op0=ALU.mult, op1=ALU.add,
                 )
-            else:
-                nc.vector.memset(base[:, 0:R], 1.0)
             if valid(i_norm):
                 nc.vector.tensor_scalar(
                     out=base[:, R:2 * R], in0=state[i_norm]["square_sum"][:], scalar1=1e-24,
                     scalar2=(4.0 if is_prototype(i_norm) else 1.0), op0=ALU.max, op1=ALU.mult,
                 )
-            else:
-                nc.vector.memset(base[:, R:2 * R], 1.0)
             inv_root = small.tile([P, 2 * R], F32, name="inv_root", tag="inv_root", bufs=depth(ROOT, HAT))
-            nc.gpsimd.tensor_tensor(out=inv_root[:], in0=base[:], in1=minus_half[:], op=ALU.pow)
+            live = slice(0 if valid(i_var) else R, 2 * R if valid(i_norm) else R)
+            nc.gpsimd.tensor_tensor(out=inv_root[:, live], in0=base[:, live], in1=minus_half[:, live], op=ALU.pow)
             if valid(i_var):
                 state[i_var]["rstd"] = inv_root[:, 0:R]
             if valid(i_norm):

from contextlib import ExitStack

from concourse import mybir
from concourse.masks import make_identity

F32 = mybir.dt.float32
BF16 = mybir.dt.bfloat16
U32 = mybir.dt.uint32
U8 = mybir.dt.uint8
FP8X4 = mybir.dt.float8_e4m3fn_x4
ALU = mybir.AluOpType
ACT = mybir.ActivationFunctionType

P = 128
K = 512
N_ROWS = 4096
CM = 512
R = 2
CHUNKS = K // P
GROUP = 4
P_ITEMS = CM // P
X_ITEMS = N_ROWS // P
ITEMS = P_ITEMS + X_ITEMS
N_GROUPS = ITEMS // GROUP
LN_EPS = 1e-5
LN_LAMDA = -4.852030263919617
SCALAR_TAIL_ITEMS = 7
VECTOR_NOISE_ITEMS = 2

EXPS = -3
NOISE = -1
MEAN = 0
AFFINE = 1
NORM = 2
ROOT = 3
HAT = 4
QUANT = 5
OUT = 6

FLOPS = 2 * (R * N_ROWS) * (R * CM) * K + 2 * N_ROWS * CM * K


def depth(first, last):
    return last - first + 2


def tile_probprotoseghead_t_kernel(tc, x, x_var, prototypes, proto_var, eps_x, eps_p, ln_w, ln_b, out):
    nc = tc.nc
    with ExitStack() as ctx:
        const = ctx.enter_context(tc.tile_pool(name="const", bufs=1))
        io = ctx.enter_context(tc.tile_pool(name="io", bufs=4))
        work = ctx.enter_context(tc.tile_pool(name="work", bufs=2))
        small = ctx.enter_context(tc.tile_pool(name="small", bufs=2))
        psum_one = ctx.enter_context(tc.psum_pool(name="psum_one", bufs=1))
        psum_two = ctx.enter_context(tc.psum_pool(name="psum_two", bufs=2))
        ctx.enter_context(tc.manual_schedule())

        x_v = x.rearrange("(p t) k -> p t k", t=X_ITEMS)
        xvar_v = x_var.rearrange("(p t) k -> p t k", t=X_ITEMS)
        ex_v = [eps_x[r].rearrange("(p t) k -> p t k", t=X_ITEMS) for r in range(R)]
        out_v = out.rearrange("(p t) c m -> p t (c m)", t=X_ITEMS)
        p_v = prototypes.rearrange("(j c) m k -> (c m) j k", j=P_ITEMS)
        pvar_v = proto_var.rearrange("(j c) m k -> (c m) j k", j=P_ITEMS)
        ep_v = [eps_p[r].rearrange("(j c) m k -> (c m) j k", j=P_ITEMS) for r in range(R)]

        w_row = const.tile([P, K], BF16, name="w_row")
        b_row = const.tile([P, K], BF16, name="b_row")
        nc.vector.memset(w_row[:], 0.0)
        nc.vector.memset(b_row[:], 0.0)
        ones_bf = const.tile([P, P], BF16, name="ones_bf")
        nc.vector.memset(ones_bf[:], 1.0)
        zero_f = const.tile([P, P], F32, name="zero_f")
        nc.vector.memset(zero_f[:], 0.0)
        minus_half = const.tile([P, 2 * R], F32, name="minus_half")
        nc.vector.memset(minus_half[:], -0.5)
        ident_bf = const.tile([P, P], BF16, name="ident_bf")
        make_identity(nc, ident_bf[:])
        ident_f = const.tile([P, P], F32, name="ident_f")
        make_identity(nc, ident_f[:])
        w_ps = psum_one.tile([P, K], F32, name="w_ps")
        b_ps = psum_one.tile([P, K], F32, name="b_ps")

        col_term = const.tile([P, CM], F32, name="col_term")
        p_codes = const.tile([P, R + 1, CM], U32, name="p_codes", align_bytes=64)
        p_scales = const.tile([P, R + 1, CM], U8, name="p_scales", align_bytes=64)

        groups = {}
        state = {}

        def valid(i):
            return 0 <= i < ITEMS

        def is_prototype(i):
            return 0 <= i < P_ITEMS

        def is_feature(i):
            return P_ITEMS <= i < ITEMS

        def load_group(g):
            var_t = io.tile([P, GROUP, K], BF16, name="var_t", tag="var_t")
            mean_t = io.tile([P, GROUP, K], BF16, name="mean_t", tag="mean_t")
            eps_t = io.tile([P, R, GROUP, K], BF16, name="eps_t", tag="eps_t")
            if g == 0:
                var_v, eps_v, mean_v, first = pvar_v, ep_v, p_v, 0
                cuts = [(0, 1), (1, GROUP)]
            else:
                var_v, eps_v, mean_v, first = xvar_v, ex_v, x_v, (g - 1) * GROUP
                cuts = [(0, GROUP)]
            for lo, hi in cuts:
                part = slice(first + lo, first + hi)
                nc.sync.dma_start(out=var_t[:, lo:hi, :], in_=var_v[:, part, :])
                for r in range(R):
                    nc.sync.dma_start(out=eps_t[:, r, lo:hi, :], in_=eps_v[r][:, part, :])
                nc.sync.dma_start(out=mean_t[:, lo:hi, :], in_=mean_v[:, part, :])
            groups[g] = {"var": var_t, "eps": eps_t, "mean": mean_t}

        def inputs(i, name):
            return groups[i // GROUP][name]

        def broadcast_gain_and_bias():
            nc.tensor.matmul(w_ps[:], lhsT=ones_bf[:], rhs=w_row[:], start=True, stop=True)
            nc.tensor.matmul(b_ps[:], lhsT=ones_bf[:], rhs=b_row[:], start=True, stop=True)

        def transpose_log_variance(i):
            words = inputs(i, "var")[:, i % GROUP, :].bitcast(F32)
            var_ps = psum_one.tile([P, K // 2], F32, name="var_ps", tag="var_ps")
            for h in range(2):
                nc.tensor.transpose(var_ps[:, h * P:(h + 1) * P], words[:, h * P:(h + 1) * P], ident_f[:])
            state[i] = {"var_ps": var_ps}

        def exps(i):
            d = state[i]
            log_var = inputs(i, "var")[:, i % GROUP, :]
            std = work.tile([P, K], F32, name="std", tag="std", bufs=depth(EXPS, NOISE))
            nc.scalar.activation(out=std[:], in_=log_var, func=ACT.Exp, scale=0.5)
            unused = work.tile([P, K], BF16, name="unused", tag="unused")
            var_sum = small.tile([P, 1], F32, name="var_sum", tag="var_sum", bufs=depth(EXPS, OUT))
            nc.scalar.activation(out=unused[:], in_=log_var, func=ACT.Exp, bias=LN_LAMDA, accum_out=var_sum[:])
            std_grouped = work.tile(
                [P, K], BF16, name="std_grouped", tag="std_grouped", bufs=depth(EXPS, QUANT), align_bytes=64
            )
            nc.scalar.activation(
                out=std_grouped[:].rearrange("p (n h e) -> p n h e", h=2, e=2),
                in_=d["var_ps"][:].bitcast(BF16).rearrange("p (h n e) -> p n h e", h=2, e=2),
                func=ACT.Exp,
                scale=0.5,
            )
            d["std"] = std
            d["var_sum"] = var_sum
            d["std_grouped"] = std_grouped

        def copy_mean_to_psum(i):
            mean_ps = psum_two.tile([P, K], F32, name="mean_ps", tag="mean_ps")
            nc.tensor.matmul(mean_ps[:], lhsT=ident_bf[:], rhs=inputs(i, "mean")[:, i % GROUP, :], start=True, stop=True)
            state[i]["mean_ps"] = mean_ps

        def noise(i):
            d = state[i]
            v = work.tile([P, R, K], F32, name="v", tag="v", bufs=depth(NOISE, AFFINE))
            engine = nc.vector if i < VECTOR_NOISE_ITEMS else nc.gpsimd
            engine.tensor_tensor(
                out=v[:],
                in0=inputs(i, "eps")[:, :, i % GROUP, :],
                in1=d["std"][:].unsqueeze(1).to_broadcast([P, R, K]),
                op=ALU.mult,
            )
            d["v"] = v
            d["row_sum"] = small.tile([P, R], F32, name="row_sum", tag="row_sum", bufs=depth(MEAN, AFFINE))

        def add_mean(i, r):
            d = state[i]
            nc.vector.scalar_tensor_tensor(
                out=d["v"][:, r, :], in0=d["v"][:, r, :], scalar=1.0, in1=d["mean_ps"][:],
                op0=ALU.mult, op1=ALU.add, accum_out=d["row_sum"][:, r:r + 1],
            )

        def squared_deviations(i):
            d = state[i]
            dev_sum = small.tile([P, R], F32, name="dev_sum", tag="dev_sum", bufs=depth(MEAN, AFFINE))
            for r in range(R):
                unused = work.tile([P, K], BF16, name="unused", tag="unused")
                nc.scalar.activation(
                    out=unused[:], in_=d["v"][:, r, :], func=ACT.Square, bias=d["row_sum"][:, r:r + 1], scale=-1.0 * K,
                    accum_out=dev_sum[:, r:r + 1],
                )
            d["dev_sum"] = dev_sum

        def roots(i_var, i_norm):
            base = small.tile([P, 2 * R], F32, name="base", tag="base")
            if valid(i_var):
                d = state[i_var]
                neg_mean = small.tile([P, R], F32, name="neg_mean", tag="neg_mean")
                nc.vector.tensor_scalar(out=neg_mean[:], in0=d["row_sum"][:], scalar1=-1.0 / K, scalar2=None, op0=ALU.mult)
                d["neg_mean"] = neg_mean
                nc.vector.tensor_scalar(
                    out=base[:, 0:R], in0=d["dev_sum"][:], scalar1=1.0 / (K * K * K), scalar2=LN_EPS,
                    op0=ALU.mult, op1=ALU.add,
                )
            if valid(i_norm):
                nc.vector.tensor_scalar(
                    out=base[:, R:2 * R], in0=state[i_norm]["square_sum"][:], scalar1=1e-24,
                    scalar2=(4.0 if is_prototype(i_norm) else 1.0), op0=ALU.max, op1=ALU.mult,
                )
            inv_root = small.tile([P, 2 * R], F32, name="inv_root", tag="inv_root", bufs=depth(ROOT, HAT))
            live = slice(0 if valid(i_var) else R, 2 * R if valid(i_norm) else R)
            nc.gpsimd.tensor_tensor(out=inv_root[:, live], in0=base[:, live], in1=minus_half[:, live], op=ALU.pow)
            if valid(i_var):
                state[i_var]["rstd"] = inv_root[:, 0:R]
            if valid(i_norm):
                state[i_norm]["inv_norm"] = inv_root[:, R:2 * R]

        def centre_and_gain(i, r):
            d = state[i]
            if r == 0:
                d["u"] = work.tile([P, R, K], F32, name="u", tag="u", bufs=depth(AFFINE, HAT))
            nc.vector.scalar_tensor_tensor(
                out=d["u"][:, r, :], in0=d["v"][:, r, :], scalar=d["neg_mean"][:, r:r + 1], in1=w_ps[:],
                op0=ALU.add, op1=ALU.mult,
            )

        def scale_and_bias(i, r):
            d = state[i]
            nc.vector.scalar_tensor_tensor(
                out=d["u"][:, r, :], in0=d["u"][:, r, :], scalar=d["rstd"][:, r:r + 1], in1=b_ps[:],
                op0=ALU.mult, op1=ALU.add,
            )

        def square_sums(i):
            d = state[i]
            square_sum = small.tile([P, R], F32, name="square_sum", tag="square_sum", bufs=depth(NORM, ROOT))
            for r in range(R):
                unused = work.tile([P, K], BF16, name="unused", tag="unused")
                nc.scalar.activation(out=unused[:], in_=d["u"][:, r, :], func=ACT.Square, accum_out=square_sum[:, r:r + 1])
            d["square_sum"] = square_sum

        def column_term_rows(i):
            repeated = work.tile([P, P], F32, name="repeated", tag="repeated")
            nc.vector.tensor_scalar(
                out=repeated[:], in0=zero_f[:], scalar1=state[i]["var_sum"][:], scalar2=-2.0,
                op0=ALU.subtract, op1=ALU.add,
            )
            term_ps = psum_one.tile([P, K // 2], F32, name="term_ps", tag="var_ps")
            nc.tensor.transpose(term_ps[:, 0:P], repeated[:], ident_f[:])
            state[i]["term_ps"] = term_ps

        def column_term_copy(i):
            nc.vector.tensor_copy(out=col_term[:, i * P:(i + 1) * P], in_=state[i]["term_ps"][:, 0:P])

        def normalise(i, r):
            d = state[i]
            if r == 0:
                d["hat"] = work.tile([P, R, K], BF16, name="hat", tag="hat")
            if i >= ITEMS - SCALAR_TAIL_ITEMS or (r == 0 and i % 3 != 2 and is_feature(i)):
                nc.scalar.activation(out=d["hat"][:, r, :], in_=d["u"][:, r, :], func=ACT.Copy, scale=d["inv_norm"][:, r:r + 1])
            else:
                nc.vector.tensor_scalar(
                    out=d["hat"][:, r, :], in0=d["u"][:, r, :], scalar1=d["inv_norm"][:, r:r + 1], scalar2=None,
                    op0=ALU.mult,
                )

        def transpose_hat(i):
            d = state[i]
            hat_ps = psum_one.tile([P, R, 2, P], F32, name="hat_ps", tag="hat_ps")
            for r in range(R):
                words = d["hat"][:, r, :].bitcast(F32)
                for h in range(2):
                    nc.tensor.transpose(hat_ps[:, r, h, :], words[:, h * P:(h + 1) * P], ident_f[:])
            d["hat_ps"] = hat_ps

        def regroup_hat(i):
            d = state[i]
            hat_grouped = work.tile(
                [P, R, P, CHUNKS], BF16, name="hat_grouped", tag="hat_grouped", bufs=depth(HAT, QUANT), align_bytes=64
            )
            nc.scalar.copy(
                out=hat_grouped[:].rearrange("p r n q -> p r (n q)").bitcast(F32).rearrange("p r (n h) -> p r n h", h=2),
                in_=d["hat_ps"][:].rearrange("p r h n -> p r n h"),
            )
            d["hat_grouped"] = hat_grouped

        def quantise(i):
            d = state[i]
            if is_prototype(i):
                cols = slice(i * P, (i + 1) * P)
                nc.vector.tensor_scalar(
                    out=d["std_grouped"][:], in0=d["std_grouped"][:], scalar1=2.0 ** -6, scalar2=None, op0=ALU.mult
                )
                for r in range(R):
                    nc.vector.quantize_mx(
                        out=p_codes[:, r, cols].bitcast(FP8X4), scales=p_scales[:, r, cols],
                        in_=d["hat_grouped"][:, r].rearrange("p n q -> p (n q)"),
                    )
                nc.vector.quantize_mx(
                    out=p_codes[:, R, cols].bitcast(FP8X4), scales=p_scales[:, R, cols], in_=d["std_grouped"][:]
                )
            else:
                codes = work.tile([P, (R + 1) * P], U32, name="codes", tag="codes", align_bytes=64)
                scales = work.tile([P, (R + 1) * P], U8, name="scales", tag="scales", align_bytes=64)
                nc.vector.quantize_mx(
                    out=codes[:, 0:R * P].bitcast(FP8X4), scales=scales[:, 0:R * P],
                    in_=d["hat_grouped"][:].rearrange("p r n q -> p (r n q)"),
                )
                nc.vector.quantize_mx(
                    out=codes[:, R * P:(R + 1) * P].bitcast(FP8X4), scales=scales[:, R * P:(R + 1) * P],
                    in_=d["std_grouped"][:],
                )
                d["codes"] = codes
                d["scales"] = scales

        def products(i):
            d = state[i]
            acc = psum_two.tile([P, CM], F32, name="acc", tag="acc")
            passes = [(r, b) for r in range(R) for b in range(R)] + [(R, R)]
            for step, (a, b) in enumerate(passes):
                nc.tensor.matmul_mx(
                    out=acc[:],
                    lhsT=d["codes"][:, a * P:(a + 1) * P].bitcast(FP8X4),
                    lhsT_scale=d["scales"][:, a * P:(a + 1) * P],
                    rhs=p_codes[:, b, :].bitcast(FP8X4),
                    rhs_scale=p_scales[:, b, :],
                    start=(step == 0),
                    stop=(step == len(passes) - 1),
                )
            d["acc"] = acc

        def output(i):
            d = state[i]
            result = work.tile([P, CM], F32, name="result", tag="result", bufs=depth(OUT, OUT + 1))
            nc.vector.scalar_tensor_tensor(
                out=result[:], in0=d["acc"][:], scalar=d["var_sum"][:], in1=col_term[:], op0=ALU.subtract, op1=ALU.add
            )
            nc.sync.dma_start(out=out_v[:, i - P_ITEMS, :], in_=result[:])

        load_group(0)
        nc.sync.dma_start(out=w_row[0:1, :], in_=ln_w.unsqueeze(0))
        nc.sync.dma_start(out=b_row[0:1, :], in_=ln_b.unsqueeze(0))
        load_group(1)
        for j in range(EXPS, ITEMS + OUT):
            i = j - EXPS
            if valid(i) and i % GROUP == 0 and i // GROUP + 2 < N_GROUPS:
                load_group(i // GROUP + 2)
            if valid(j - EXPS):
                transpose_log_variance(j - EXPS)
            if valid(j - NOISE):
                copy_mean_to_psum(j - NOISE)
            if j == NOISE:
                broadcast_gain_and_bias()
            if valid(j - HAT):
                normalise(j - HAT, 0)
                normalise(j - HAT, 1)
                transpose_hat(j - HAT)
            if valid(j - QUANT):
                quantise(j - QUANT)
            if is_feature(j - QUANT):
                products(j - QUANT)
            if valid(j - AFFINE) or valid(j - ROOT):
                roots(j - AFFINE, j - ROOT)
            if valid(j - EXPS):
                exps(j - EXPS)
            if valid(j - NORM):
                square_sums(j - NORM)
            if valid(j - NOISE):
                noise(j - NOISE)
            if is_prototype(j - NORM):
                column_term_rows(j - NORM)
            if valid(j - HAT):
                regroup_hat(j - HAT)
            if valid(j - MEAN):
                add_mean(j - MEAN, 0)
                add_mean(j - MEAN, 1)
            if valid(j - AFFINE):
                centre_and_gain(j - AFFINE, 0)
                centre_and_gain(j - AFFINE, 1)
                scale_and_bias(j - AFFINE, 0)
                scale_and_bias(j - AFFINE, 1)
            if is_feature(j - OUT):
                output(j - OUT)
            if is_prototype(j - NORM):
                column_term_copy(j - NORM)
            if valid(j - MEAN):
                squared_deviations(j - MEAN)
